import numpy as np
import ml_dtypes


def mxq(x, axis, fmt="e4m3"):
    dtype, down = {"e4m3": (ml_dtypes.float8_e4m3fn, 7), "e5m2": (ml_dtypes.float8_e5m2, 14)}[fmt]
    v = np.moveaxis(np.asarray(x, np.float32).astype(ml_dtypes.bfloat16).astype(np.float64), axis, -1)
    blocks = v.reshape(v.shape[:-1] + (-1, 32))
    amax = np.abs(blocks).max(-1, keepdims=True)
    byte = np.maximum(np.where(amax > 0, np.frexp(amax)[1] - 1 + 127, 0) - down, 1)
    scale = np.exp2(byte - 127.0)
    codes = (blocks / scale).astype(np.float32).astype(dtype).astype(np.float64)
    return np.moveaxis((codes * scale).reshape(v.shape), -1, axis)


WIDE = False


def mx_kscale(k):
    if not WIDE:
        return np.ones(k)
    levels = np.array([10, -10, 5, -5, 0])
    a = np.random.permutation(np.resize(levels, k // 512 * 4)).reshape(k // 512, 4)
    idx = np.arange(k)
    return np.exp2(a[idx // 512, idx % 128 // 32])


BF16 = ml_dtypes.bfloat16


def bf(x):
    return np.asarray(x, np.float32).astype(BF16)


def f64(x):
    return np.asarray(x).astype(np.float64)


E2M1 = np.array([0.0, 0.5, 1.0, 1.5, 2.0, 3.0, 4.0, 6.0, -0.0, -0.5, -1.0, -1.5, -2.0, -3.0, -4.0, -6.0])


def pack_weight(w, fmt):
    k, n = w.shape
    w = f64(bf(w)).reshape(k // 32, 32, n)
    amax = np.abs(w).max(1)
    if fmt == "e4m3":
        byte = np.frexp(amax)[1] - 1 + 127 - 7
    else:
        mant, ex = np.frexp(amax / 6.0)
        byte = np.where(mant > 0.5, ex, ex - 1) + 127
    byte = np.clip(np.where(amax > 0, byte, 1), 1, 254)
    scaled = (w * np.exp2(127.0 - byte)[:, None, :]).reshape(k, n).astype(np.float32)
    by_word = np.ascontiguousarray(scaled.reshape(k // 512, 128, 4, n).transpose(0, 1, 3, 2))
    if fmt == "e4m3":
        words = by_word.astype(ml_dtypes.float8_e4m3fn).view(np.uint8)
    else:
        c = by_word.astype(ml_dtypes.float4_e2m1fn).view(np.uint8) & 0xF
        words = c[..., 0::2] | (c[..., 1::2] << 4)
    return np.ascontiguousarray(words), np.ascontiguousarray(byte.astype(np.uint8).reshape(k // 512, 16, n))


def unpack_weight(words, scales, fmt):
    g, p, n, _ = words.shape
    if fmt == "e4m3":
        vals = np.ascontiguousarray(words).view(ml_dtypes.float8_e4m3fn).astype(np.float64)
    else:
        nib = np.empty((g, p, n, 4), np.uint8)
        nib[..., 0::2] = words & 0xF
        nib[..., 1::2] = words >> 4
        vals = E2M1[nib]
    vals = vals * np.repeat(np.exp2(scales.astype(np.float64) - 127.0), 8, axis=1)[..., None]
    return vals.transpose(0, 1, 3, 2).reshape(g * 512, n)


B, H, W, D, Dh, Dq, R, T = 4, 16, 16, 1024, 1024, 128, 16, 8
EPS = 1e-6
FMT = "e4m3"


def layer_norm(v, g, b):
    mu = v.mean(-1, keepdims=True)
    var = ((v - mu) ** 2).mean(-1, keepdims=True)
    return (v - mu) / np.sqrt(var + EPS) * g + b


def setup_inputs():
    rn = np.random.standard_normal
    s, t = mx_kscale(D), mx_kscale(Dh)
    x = bf(rn((B, H, W, D)) * s)
    z2 = bf(rn((B, H, W, Dq)) * 1.5)
    U1_w_words, U1_w_scales = pack_weight(np.ascontiguousarray((rn((Dh, D)) * np.sqrt(2.0 / D) / s).T), FMT)
    U1_b = bf(rn(Dh) * 0.5)
    U3_w = bf(rn((Dh, Dq)) * np.sqrt(2.0 / Dq))
    U3_b = bf(rn(Dh) * 0.5)
    C_w_words, C_w_scales = pack_weight(np.ascontiguousarray((rn((D, Dh)) / np.sqrt(Dh) / t).T), FMT)
    return {
        "x": x,
        "z2": z2,
        "U1_w_words": U1_w_words,
        "U1_w_scales": U1_w_scales,
        "U1_b": U1_b,
        "U3_w": U3_w,
        "U3_b": U3_b,
        "C_w_words": C_w_words,
        "C_w_scales": C_w_scales,
        "C_b": bf(rn(D) * 0.3),
        "ln1_g": bf((1.0 + 0.1 * rn(Dh)) * t),
        "ln1_b": bf(0.2 * rn(Dh) * t),
        "ln3_g": bf(1.0 + 0.1 * rn(Dh)),
        "ln3_b": bf(0.2 * rn(Dh)),
        "alpha": bf(0.6 + 0.2 * np.random.random(1)),
    }


def reference(x, z2, U1_w_words, U1_w_scales, U1_b, U3_w, U3_b, C_w_words, C_w_scales, C_b, ln1_g, ln1_b, ln3_g, ln3_b, alpha):
    out1 = (mxq(f64(x), 3, "e4m3") @ unpack_weight(U1_w_words, U1_w_scales, FMT)) + f64(U1_b)
    out3 = f64(z2) @ f64(U3_w).T + f64(U3_b)
    o1 = layer_norm(out1, f64(ln1_g), f64(ln1_b))
    o3 = layer_norm(out3, f64(ln3_g), f64(ln3_b))
    h = o1 + f64(alpha) * (o1 * o3)
    return (mxq(h, 3, "e4m3") @ unpack_weight(C_w_words, C_w_scales, FMT)) + f64(C_b)

@@ -1,0 +1,341 @@
+from contextlib import ExitStack
+
+import concourse.mybir as mybir
+from concourse.masks import make_identity
+
+F32 = mybir.dt.float32
+BF16 = mybir.dt.bfloat16
+I32 = mybir.dt.int32
+U32 = mybir.dt.uint32
+U8 = mybir.dt.uint8
+FP8X4 = mybir.dt.float8_e4m3fn_x4
+ALU = mybir.AluOpType
+ACT = mybir.ActivationFunctionType
+
+P = 128
+PACK = 4
+K_PASS = P * PACK
+BANK = 512
+
+TOKENS = 1024
+D = 1024
+DH = 1024
+DQ = 128
+EPS = 1e-6
+
+TOKEN_TILES = TOKENS // P
+PASSES = DH // K_PASS
+GROUP = 4
+GROUPS = TOKEN_TILES // GROUP
+
+FLOPS = 2 * TOKENS * (D * DH + DQ * DH + DH * D)
+
+
+def tile_polymlp_skiplora_pa_kernel(
+    tc,
+    x,
+    z2,
+    U1_w_words,
+    U1_w_scales,
+    U1_b,
+    U3_w,
+    U3_b,
+    C_w_words,
+    C_w_scales,
+    C_b,
+    ln1_g,
+    ln1_b,
+    ln3_g,
+    ln3_b,
+    alpha,
+    out,
+):
+    nc = tc.nc
+    x_rows = x.flatten_outer_dims()
+    z2_rows = z2.flatten_outer_dims()
+    out_rows = out.flatten_outer_dims()
+
+    with ExitStack() as stack:
+        keep = stack.enter_context(tc.tile_pool(name="keep", bufs=1))
+        stage = stack.enter_context(tc.tile_pool(name="stage", bufs=2))
+        acc = stack.enter_context(tc.psum_pool(name="acc", bufs=4))
+        tp = stack.enter_context(tc.psum_pool(name="tp", bufs=4))
+
+        stack.enter_context(tc.manual_schedule())
+
+        planes = keep.tile([P, D], U8, align_bytes=64)
+        nc.vector.memset(planes[:].bitcast(I32), 0)
+
+        def load_scales(scales_dram, first_plane):
+            for quadrant in range(4):
+                first_row = 32 * quadrant + 4 * first_plane
+                nc.sync.dma_start(
+                    out=planes[first_row : first_row + 4 * PASSES, :].bitcast(I32),
+                    in_=scales_dram[:, 4 * quadrant : 4 * quadrant + 4, :].bitcast(I32),
+                )
+
+        def load_words(words_dram, name):
+            words_sb = keep.tile([P, PASSES, PACK * DH], U8, align_bytes=64, name=name)
+            for g in range(PASSES):
+                nc.sync.dma_start(
+                    out=words_sb[:, g, :].bitcast(I32),
+                    in_=words_dram[g].rearrange("p n t -> p (n t)").bitcast(I32),
+                )
+            return words_sb
+
+        def load_broadcast(vector, name):
+            raw = keep.tile([P, DH], BF16, name=name)
+            nc.sync.dma_start(out=raw[:], in_=vector.partition_broadcast(P))
+            return raw
+
+        x_sb = keep.tile([P, TOKEN_TILES, D], BF16)
+
+        def load_x(i):
+            nc.sync.dma_start(out=x_sb[:, i, :], in_=x_rows[i * P : (i + 1) * P, :])
+
+        z2_sb = keep.tile([P, TOKEN_TILES, DQ], BF16)
+        nc.sync.dma_start(out=z2_sb[:], in_=z2_rows.rearrange("(i p) d -> p i d", p=P))
+        u3_sb = keep.tile([P, PASSES, PACK, DQ], BF16)
+        nc.sync.dma_start(
+            out=u3_sb[:], in_=U3_w.rearrange("(g p t) d -> p g t d", g=PASSES, t=PACK)
+        )
+        u3_b_raw = load_broadcast(U3_b, "u3_b_raw")
+        u1_b_raw = load_broadcast(U1_b, "u1_b_raw")
+        load_scales(U1_w_scales, 0)
+        load_x(0)
+        w1_words = load_words(U1_w_words, "w1_words")
+        for i in range(1, GROUP):
+            load_x(i)
+        ln_raw = keep.tile([P, 4, 16], BF16)
+        for v, vector in enumerate((ln1_g, ln1_b, ln3_g, ln3_b)):
+            nc.sync.dma_start(
+                out=ln_raw[:, v, 0 : PASSES * PACK].rearrange("p (g t) -> p g t", g=PASSES),
+                in_=vector.rearrange("(g p t) -> p g t", g=PASSES, t=PACK),
+            )
+        alpha_raw = keep.tile([P, 1], BF16)
+        nc.sync.dma_start(out=alpha_raw[:], in_=alpha.partition_broadcast(P))
+        for i in range(GROUP, TOKEN_TILES):
+            load_x(i)
+        load_scales(C_w_scales, PASSES)
+        c_words = load_words(C_w_words, "c_words")
+        c_b = load_broadcast(C_b, "c_b")
+
+        ident_f32 = keep.tile([P, P], F32)
+        make_identity(nc, ident_f32[:])
+        ident_bf16 = keep.tile([P, P], BF16)
+        make_identity(nc, ident_bf16[:])
+        eps = keep.tile([P, 1], F32)
+        nc.vector.memset(eps[:], EPS)
+
+        z2T_ps = tp.tile([P, TOKENS], BF16, tag="tp")
+        for i in range(TOKEN_TILES):
+            nc.tensor.transpose(z2T_ps[:, i * P : (i + 1) * P], z2_sb[:, i, :], ident_bf16[:])
+        z2T = keep.tile([P, TOKENS], BF16)
+        nc.vector.tensor_copy(out=z2T[:], in_=z2T_ps[:])
+        u3T_ps = tp.tile([P, PASSES, PACK, P], BF16, tag="tp")
+        for g in range(PASSES):
+            for t in range(PACK):
+                nc.tensor.transpose(u3T_ps[:, g, t, :], u3_sb[:, g, t, :], ident_bf16[:])
+        u3T = keep.tile([P, PASSES, PACK * P], BF16)
+        nc.scalar.copy(out=u3T[:], in_=u3T_ps[:].rearrange("d g t p -> d g (t p)"))
+
+        u3_b = keep.tile([P, PASSES, PACK, P], F32)
+        nc.vector.tensor_copy(
+            out=u3_b[:], in_=u3_b_raw[:].rearrange("q (g p t) -> q g t p", g=PASSES, t=PACK)
+        )
+        u1_b = keep.tile([P, PASSES, PACK, P], F32)
+
+        def spread_u1_b():
+            nc.scalar.copy(
+                out=u1_b[:], in_=u1_b_raw[:].rearrange("q (g p t) -> q g t p", g=PASSES, t=PACK)
+            )
+
+        affine = keep.tile([P, 4, PASSES * PACK], F32)
+
+        def gains_and_shifts():
+            alpha_f32 = keep.tile([P, 1], F32)
+            nc.vector.tensor_copy(out=alpha_f32[:], in_=alpha_raw[:])
+            ln_cols = ln_raw[:, :, 0 : PASSES * PACK]
+            nc.vector.tensor_copy(out=affine[:, 0:2, :], in_=ln_cols[:, 0:2, :])
+            nc.vector.tensor_scalar(
+                out=affine[:, 2, :], in0=ln_cols[:, 2, :], scalar1=alpha_f32[:, 0:1], scalar2=None,
+                op0=ALU.mult,
+            )
+            nc.vector.tensor_scalar(
+                out=affine[:, 3, :], in0=ln_cols[:, 3, :], scalar1=alpha_f32[:, 0:1], scalar2=1.0,
+                op0=ALU.mult, op1=ALU.add,
+            )
+
+        x_codes = keep.tile([P, TOKEN_TILES, PASSES, P], U32, align_bytes=64)
+        x_scales = keep.tile([P, TOKEN_TILES, PASSES, P], U8, align_bytes=64)
+        h_codes = keep.tile([P, GROUPS, PASSES, GROUP * P], U32, align_bytes=64)
+        h_scales = keep.tile([P, GROUPS, PASSES, GROUP * P], U8, align_bytes=64)
+
+        def turn_x(i):
+            words = x_sb[:, i, :].bitcast(F32)
+            xT = tp.tile([P, PASSES, 2, P], F32, tag="tp")
+            for g in range(PASSES):
+                for u in range(2):
+                    first = (K_PASS // 2) * g + u
+                    nc.tensor.transpose(
+                        xT[:, g, u, :], words[:, first : (K_PASS // 2) * (g + 1) : 2], ident_f32[:]
+                    )
+            grouped = stage.tile([P, PASSES, P, PACK], BF16, align_bytes=64, name="x_grouped")
+            nc.scalar.copy(out=grouped[:].bitcast(F32), in_=xT[:].rearrange("p g u w -> p g w u"))
+            return grouped
+
+        def quantise_x(i, grouped):
+            nc.vector.quantize_mx(
+                out=x_codes[:, i].rearrange("p g w -> p (g w)").bitcast(FP8X4),
+                scales=x_scales[:, i].rearrange("p g w -> p (g w)"),
+                in_=grouped[:].rearrange("p g w t -> p (g w t)"),
+            )
+
+        def start_norm(banks, pattern, bias, name):
+            rows = keep.tile([P, PASSES, PACK, P], F32, name=name)
+            sums = stage.tile([P, PASSES], F32, name="sums", bufs=4)
+            for g in range(PASSES):
+                nc.vector.scalar_tensor_tensor(
+                    out=rows[:, g], in0=banks[g][:].rearrange(pattern, t=PACK), scalar=1.0,
+                    in1=bias[:, g], op0=ALU.mult, op1=ALU.add, accum_out=sums[:, g : g + 1],
+                )
+            neg_mean = stage.tile([P, 1], F32, name="neg_mean", bufs=4)
+            nc.vector.tensor_scalar(
+                out=neg_mean[:], in0=sums[:, 0:1], scalar1=sums[:, 1:2], scalar2=-1.0 / DH,
+                op0=ALU.add, op1=ALU.mult,
+            )
+            squares = stage.tile([P, DH], BF16, name="squares", bufs=4)
+            sum_sq = stage.tile([P, 1], F32, name="sum_sq", bufs=4)
+            nc.scalar.activation(
+                out=squares[:], in_=rows[:].rearrange("q g t p -> q (g t p)"), func=ACT.Square,
+                bias=neg_mean[:, 0:1], scale=1.0, accum_out=sum_sq[:, 0:1],
+            )
+            std = stage.tile([P, 1], F32, name="std", bufs=4)
+            nc.scalar.activation(
+                out=std[:], in_=sum_sq[:], func=ACT.Sqrt, bias=eps[:, 0:1], scale=1.0 / DH
+            )
+            return rows, neg_mean, std
+
+        def finish_norm(rows, neg_mean, std):
+            rstd = stage.tile([P, 1], F32, name="rstd", bufs=4)
+            nc.vector.reciprocal(out=rstd[:], in_=std[:])
+            flat = rows[:].rearrange("q g t p -> q (g t p)")
+            nc.vector.tensor_scalar(
+                out=flat, in0=flat, scalar1=neg_mean[:, 0:1], scalar2=rstd[:, 0:1],
+                op0=ALU.add, op1=ALU.mult,
+            )
+
+        def start_branch3(i):
+            banks = [acc.tile([P, BANK], F32, name="y3_%d" % g, tag="acc") for g in range(PASSES)]
+            for g in range(PASSES):
+                nc.tensor.matmul(
+                    out=banks[g][:], lhsT=z2T[:, i * P : (i + 1) * P], rhs=u3T[:, g, :],
+                    start=True, stop=True,
+                )
+            return start_norm(banks, "q (t p) -> q t p", u3_b, "u3_%d" % i)
+
+        def mx_product(codes, scales, weight_words, first_plane, name):
+            banks = [acc.tile([P, BANK], F32, name="%s_%d" % (name, n), tag="acc") for n in range(2)]
+            for g in range(PASSES):
+                plane_row = 4 * (first_plane + g)
+                for n in range(2):
+                    nc.tensor.matmul_mx(
+                        out=banks[n][:],
+                        lhsT=codes[:, g, :].bitcast(FP8X4),
+                        lhsT_scale=scales[:, g, :],
+                        rhs=weight_words[:, g, PACK * BANK * n : PACK * BANK * (n + 1)].bitcast(FP8X4),
+                        rhs_scale=planes[plane_row:P, BANK * n : BANK * (n + 1)],
+                        start=(g == 0),
+                        stop=(g == PASSES - 1),
+                    )
+            return banks
+
+        def start_branch1(i):
+            banks = mx_product(x_codes[:, i], x_scales[:, i], w1_words, 0, "y1")
+            return start_norm(banks, "q (p t) -> q t p", u1_b, "u1_%d" % i)
+
+        def turn_and_scale(rows, factor, b, g, t):
+            turned = tp.tile([P, GROUP * P], F32, name="turned", tag="tp")
+            for j in range(GROUP):
+                nc.tensor.transpose(turned[:, j * P : (j + 1) * P], rows[j][:, g, t, :], ident_f32[:])
+            column = g * PACK + t
+            nc.scalar.activation(
+                out=factor[:, t, :], in_=turned[:], func=ACT.Identity,
+                scale=affine[:, 2 * b, column : column + 1],
+                bias=affine[:, 2 * b + 1, column : column + 1],
+            )
+
+        def multiply(grp, g, factors):
+            grouped = stage.tile([P, GROUP * P, PACK], BF16, align_bytes=64, name="h_grouped")
+            nc.vector.tensor_tensor(
+                out=grouped[:],
+                in0=factors[0][:].rearrange("p t w -> p w t"),
+                in1=factors[1][:].rearrange("p t w -> p w t"),
+                op=ALU.mult,
+            )
+            nc.vector.quantize_mx(
+                out=h_codes[:, grp, g, :].bitcast(FP8X4),
+                scales=h_scales[:, grp, g, :],
+                in_=grouped[:].rearrange("p w t -> p (w t)"),
+            )
+
+        def project(grp, j):
+            tokens = slice(j * P, (j + 1) * P)
+            banks = mx_product(
+                h_codes[:, grp, :, tokens], h_scales[:, grp, :, tokens], c_words, PASSES, "y2"
+            )
+            result = stage.tile([P, D], F32, name="result", bufs=3)
+            for n in range(2):
+                nc.vector.tensor_tensor(
+                    out=result[:, BANK * n : BANK * (n + 1)], in0=banks[n][:],
+                    in1=c_b[:, BANK * n : BANK * (n + 1)], op=ALU.add,
+                )
+            i = grp * GROUP + j
+            nc.sync.dma_start(out=out_rows[i * P : (i + 1) * P, :], in_=result[:])
+
+        quantise_x(0, turn_x(0))
+        spread_u1_b()
+        rows = {1: [], 3: []}
+        factors = {}
+        waiting = None
+        for r in range(GROUPS + 2):
+            for j in range(GROUP):
+                if r < GROUPS:
+                    i = r * GROUP + j
+                    unit = start_branch3(i)
+                    rows[3].append(unit[0])
+                    if waiting is not None:
+                        finish_norm(*waiting)
+                    waiting = unit
+                    if i + 1 < TOKEN_TILES:
+                        grouped = turn_x(i + 1)
+                    unit = start_branch1(i)
+                    rows[1].append(unit[0])
+                    finish_norm(*waiting)
+                    waiting = unit
+                    if i + 1 < TOKEN_TILES:
+                        quantise_x(i + 1, grouped)
+                elif waiting is not None:
+                    finish_norm(*waiting)
+                    waiting = None
+                if 1 <= r <= GROUPS:
+                    grp = r - 1
+                    if r == 1 and j == 0:
+                        gains_and_shifts()
+                    g = j // 2
+                    if j % 2 == 0:
+                        factors[(grp, g)] = [
+                            stage.tile([P, PACK, GROUP * P], F32, name="factor_%d" % b) for b in range(2)
+                        ]
+                    if j == 2:
+                        multiply(grp, 0, factors[(grp, 0)])
+                    for t in (2 * (j % 2), 2 * (j % 2) + 1):
+                        for b, branch in enumerate((1, 3)):
+                            turn_and_scale(
+                                rows[branch][grp * GROUP : (grp + 1) * GROUP], factors[(grp, g)][b], b, g, t
+                            )
+                if r >= 2:
+                    grp = r - 2
+                    if j == 0:
+                        multiply(grp, 1, factors[(grp, 1)])
+                    project(grp, j)

@@ -27,6 +27,9 @@ TOKEN_TILES = TOKENS // P
 PASSES = DH // K_PASS
 GROUP = 4
 GROUPS = TOKEN_TILES // GROUP
+NORM_LAG = 2
+GATE_LAG = GROUP + 1
+PROJECT_LAG = GATE_LAG + 4
 
 FLOPS = 2 * TOKENS * (D * DH + DQ * DH + DH * D)
 
@@ -63,6 +66,11 @@ def tile_polymlp_skiplora_pa_kernel(
 
         stack.enter_context(tc.manual_schedule())
 
+        bias_rows = keep.tile([P, 3, DH], BF16)
+        nc.vector.memset(bias_rows[:].bitcast(I32), 0)
+        for v, vector in enumerate((U3_b, U1_b, C_b)):
+            nc.sync.dma_start(out=bias_rows[0:1, v, :], in_=vector.rearrange("(o n) -> o n", o=1))
+
         planes = keep.tile([P, D], U8, align_bytes=64)
         nc.vector.memset(planes[:].bitcast(I32), 0)
 
@@ -83,11 +91,6 @@ def tile_polymlp_skiplora_pa_kernel(
                 )
             return words_sb
 
-        def load_broadcast(vector, name):
-            raw = keep.tile([P, DH], BF16, name=name)
-            nc.sync.dma_start(out=raw[:], in_=vector.partition_broadcast(P))
-            return raw
-
         x_sb = keep.tile([P, TOKEN_TILES, D], BF16)
 
         def load_x(i):
@@ -99,8 +102,6 @@ def tile_polymlp_skiplora_pa_kernel(
         nc.sync.dma_start(
             out=u3_sb[:], in_=U3_w.rearrange("(g p t) d -> p g t d", g=PASSES, t=PACK)
         )
-        u3_b_raw = load_broadcast(U3_b, "u3_b_raw")
-        u1_b_raw = load_broadcast(U1_b, "u1_b_raw")
         load_scales(U1_w_scales, 0)
         load_x(0)
         w1_words = load_words(U1_w_words, "w1_words")
@@ -118,14 +119,27 @@ def tile_polymlp_skiplora_pa_kernel(
             load_x(i)
         load_scales(C_w_scales, PASSES)
         c_words = load_words(C_w_words, "c_words")
-        c_b = load_broadcast(C_b, "c_b")
 
         ident_f32 = keep.tile([P, P], F32)
         make_identity(nc, ident_f32[:])
         ident_bf16 = keep.tile([P, P], BF16)
         make_identity(nc, ident_bf16[:])
+        ones = keep.tile([P, P], BF16)
+        nc.vector.memset(ones[:], 1.0)
         eps = keep.tile([P, 1], F32)
         nc.vector.memset(eps[:], EPS)
+
+        def spread_bias(v, spread, pattern):
+            for n in range(2):
+                bank = acc.tile([P, BANK], F32, name="bias_bank", tag="acc")
+                nc.tensor.matmul(
+                    out=bank[:], lhsT=ones[:], rhs=bias_rows[:, v, BANK * n : BANK * (n + 1)],
+                    start=True, stop=True,
+                )
+                if n == 0:
+                    nc.vector.tensor_copy(out=spread[:, n], in_=bank[:].rearrange(pattern, t=PACK))
+                else:
+                    nc.scalar.copy(out=spread[:, n], in_=bank[:].rearrange(pattern, t=PACK))
 
         z2T_ps = tp.tile([P, TOKENS], BF16, tag="tp")
         for i in range(TOKEN_TILES):
@@ -140,15 +154,10 @@ def tile_polymlp_skiplora_pa_kernel(
         nc.scalar.copy(out=u3T[:], in_=u3T_ps[:].rearrange("d g t p -> d g (t p)"))
 
         u3_b = keep.tile([P, PASSES, PACK, P], F32)
-        nc.vector.tensor_copy(
-            out=u3_b[:], in_=u3_b_raw[:].rearrange("q (g p t) -> q g t p", g=PASSES, t=PACK)
-        )
+        spread_bias(0, u3_b, "q (p t) -> q t p")
         u1_b = keep.tile([P, PASSES, PACK, P], F32)
-
-        def spread_u1_b():
-            nc.scalar.copy(
-                out=u1_b[:], in_=u1_b_raw[:].rearrange("q (g p t) -> q g t p", g=PASSES, t=PACK)
-            )
+        spread_bias(1, u1_b, "q (p t) -> q t p")
+        c_b = keep.tile([P, 2, PACK, P], F32)
 
         affine = keep.tile([P, 4, PASSES * PACK], F32)
 
@@ -191,49 +200,6 @@ def tile_polymlp_skiplora_pa_kernel(
                 in_=grouped[:].rearrange("p g w t -> p (g w t)"),
             )
 
-        def start_norm(banks, pattern, bias, name):
-            rows = keep.tile([P, PASSES, PACK, P], F32, name=name)
-            sums = stage.tile([P, PASSES], F32, name="sums", bufs=4)
-            for g in range(PASSES):
-                nc.vector.scalar_tensor_tensor(
-                    out=rows[:, g], in0=banks[g][:].rearrange(pattern, t=PACK), scalar=1.0,
-                    in1=bias[:, g], op0=ALU.mult, op1=ALU.add, accum_out=sums[:, g : g + 1],
-                )
-            neg_mean = stage.tile([P, 1], F32, name="neg_mean", bufs=4)
-            nc.vector.tensor_scalar(
-                out=neg_mean[:], in0=sums[:, 0:1], scalar1=sums[:, 1:2], scalar2=-1.0 / DH,
-                op0=ALU.add, op1=ALU.mult,
-            )
-            squares = stage.tile([P, DH], BF16, name="squares", bufs=4)
-            sum_sq = stage.tile([P, 1], F32, name="sum_sq", bufs=4)
-            nc.scalar.activation(
-                out=squares[:], in_=rows[:].rearrange("q g t p -> q (g t p)"), func=ACT.Square,
-                bias=neg_mean[:, 0:1], scale=1.0, accum_out=sum_sq[:, 0:1],
-            )
-            std = stage.tile([P, 1], F32, name="std", bufs=4)
-            nc.scalar.activation(
-                out=std[:], in_=sum_sq[:], func=ACT.Sqrt, bias=eps[:, 0:1], scale=1.0 / DH
-            )
-            return rows, neg_mean, std
-
-        def finish_norm(rows, neg_mean, std):
-            rstd = stage.tile([P, 1], F32, name="rstd", bufs=4)
-            nc.vector.reciprocal(out=rstd[:], in_=std[:])
-            flat = rows[:].rearrange("q g t p -> q (g t p)")
-            nc.vector.tensor_scalar(
-                out=flat, in0=flat, scalar1=neg_mean[:, 0:1], scalar2=rstd[:, 0:1],
-                op0=ALU.add, op1=ALU.mult,
-            )
-
-        def start_branch3(i):
-            banks = [acc.tile([P, BANK], F32, name="y3_%d" % g, tag="acc") for g in range(PASSES)]
-            for g in range(PASSES):
-                nc.tensor.matmul(
-                    out=banks[g][:], lhsT=z2T[:, i * P : (i + 1) * P], rhs=u3T[:, g, :],
-                    start=True, stop=True,
-                )
-            return start_norm(banks, "q (t p) -> q t p", u3_b, "u3_%d" % i)
-
         def mx_product(codes, scales, weight_words, first_plane, name):
             banks = [acc.tile([P, BANK], F32, name="%s_%d" % (name, n), tag="acc") for n in range(2)]
             for g in range(PASSES):
@@ -250,27 +216,82 @@ def tile_polymlp_skiplora_pa_kernel(
                     )
             return banks
 
-        def start_branch1(i):
-            banks = mx_product(x_codes[:, i], x_scales[:, i], w1_words, 0, "y1")
-            return start_norm(banks, "q (p t) -> q t p", u1_b, "u1_%d" % i)
+        def branch_product(branch, i):
+            if branch == 1:
+                return mx_product(x_codes[:, i], x_scales[:, i], w1_words, 0, "y1")
+            banks = [acc.tile([P, BANK], F32, name="y3_%d" % g, tag="acc") for g in range(PASSES)]
+            for g in range(PASSES):
+                nc.tensor.matmul(
+                    out=banks[g][:], lhsT=z2T[:, i * P : (i + 1) * P], rhs=u3T[:, g, :],
+                    start=True, stop=True,
+                )
+            return banks
 
-        def turn_and_scale(rows, factor, b, g, t):
+        rows = {}
+        stats = {}
+
+        def add_bias(branch, i):
+            banks = branch_product(branch, i)
+            pattern = "q (p t) -> q t p" if branch == 1 else "q (t p) -> q t p"
+            bias = u1_b if branch == 1 else u3_b
+            rows[(branch, i)] = keep.tile([P, PASSES, PACK, P], F32, name="rows_%d_%d" % (branch, i))
+            stats[(branch, i)] = [
+                stage.tile([P, width], F32, name=name, bufs=6)
+                for name, width in (("sums", PASSES), ("neg_mean", 1), ("sum_sq", 1), ("std", 1), ("rstd", 1))
+            ]
+            sums = stats[(branch, i)][0]
+            for g in range(PASSES):
+                nc.vector.scalar_tensor_tensor(
+                    out=rows[(branch, i)][:, g], in0=banks[g][:].rearrange(pattern, t=PACK), scalar=1.0,
+                    in1=bias[:, g], op0=ALU.mult, op1=ALU.add, accum_out=sums[:, g : g + 1],
+                )
+
+        def deviation(branch, i):
+            sums, neg_mean, sum_sq, std, rstd = stats[(branch, i)]
+            nc.vector.tensor_scalar(
+                out=neg_mean[:], in0=sums[:, 0:1], scalar1=sums[:, 1:2], scalar2=-1.0 / DH,
+                op0=ALU.add, op1=ALU.mult,
+            )
+            squares = stage.tile([P, DH], BF16, name="squares", bufs=4)
+            nc.scalar.activation(
+                out=squares[:], in_=rows[(branch, i)][:].rearrange("q g t p -> q (g t p)"),
+                func=ACT.Square, bias=neg_mean[:, 0:1], scale=1.0, accum_out=sum_sq[:, 0:1],
+            )
+            nc.scalar.activation(
+                out=std[:], in_=sum_sq[:], func=ACT.Sqrt, bias=eps[:, 0:1], scale=1.0 / DH
+            )
+
+        def invert(branch, i):
+            sums, neg_mean, sum_sq, std, rstd = stats[(branch, i)]
+            nc.vector.reciprocal(out=rstd[:], in_=std[:])
+
+        def normalise(branch, i):
+            sums, neg_mean, sum_sq, std, rstd = stats[(branch, i)]
+            flat = rows[(branch, i)][:].rearrange("q g t p -> q (g t p)")
+            nc.vector.tensor_scalar(
+                out=flat, in0=flat, scalar1=neg_mean[:, 0:1], scalar2=rstd[:, 0:1],
+                op0=ALU.add, op1=ALU.mult,
+            )
+
+        def turn_and_scale(grp, factor, branch, g, t):
             turned = tp.tile([P, GROUP * P], F32, name="turned", tag="tp")
             for j in range(GROUP):
-                nc.tensor.transpose(turned[:, j * P : (j + 1) * P], rows[j][:, g, t, :], ident_f32[:])
+                nc.tensor.transpose(
+                    turned[:, j * P : (j + 1) * P], rows[(branch, grp * GROUP + j)][:, g, t, :], ident_f32[:]
+                )
             column = g * PACK + t
             nc.scalar.activation(
                 out=factor[:, t, :], in_=turned[:], func=ACT.Identity,
-                scale=affine[:, 2 * b, column : column + 1],
-                bias=affine[:, 2 * b + 1, column : column + 1],
+                scale=affine[:, branch - 1, column : column + 1],
+                bias=affine[:, branch, column : column + 1],
             )
 
         def multiply(grp, g, factors):
             grouped = stage.tile([P, GROUP * P, PACK], BF16, align_bytes=64, name="h_grouped")
             nc.vector.tensor_tensor(
-                out=grouped[:],
-                in0=factors[0][:].rearrange("p t w -> p w t"),
-                in1=factors[1][:].rearrange("p t w -> p w t"),
+                out=grouped[:].rearrange("p (c i) t -> p c t i", i=4),
+                in0=factors[0][:].rearrange("p t (c i) -> p c t i", i=4),
+                in1=factors[1][:].rearrange("p t (c i) -> p c t i", i=4),
                 op=ALU.mult,
             )
             nc.vector.quantize_mx(
@@ -284,58 +305,60 @@ def tile_polymlp_skiplora_pa_kernel(
             banks = mx_product(
                 h_codes[:, grp, :, tokens], h_scales[:, grp, :, tokens], c_words, PASSES, "y2"
             )
-            result = stage.tile([P, D], F32, name="result", bufs=3)
+            result = stage.tile([P, 2, BANK], F32, name="result", bufs=3)
             for n in range(2):
                 nc.vector.tensor_tensor(
-                    out=result[:, BANK * n : BANK * (n + 1)], in0=banks[n][:],
-                    in1=c_b[:, BANK * n : BANK * (n + 1)], op=ALU.add,
+                    out=result[:, n, :], in0=banks[n][:],
+                    in1=c_b[:, n].rearrange("q t p -> q (t p)"), op=ALU.add,
                 )
             i = grp * GROUP + j
-            nc.sync.dma_start(out=out_rows[i * P : (i + 1) * P, :], in_=result[:])
+            nc.sync.dma_start(
+                out=out_rows[i * P : (i + 1) * P, :], in_=result[:].rearrange("q n c -> q (n c)")
+            )
+
+        units = [(branch, i) for i in range(TOKEN_TILES) for branch in (3, 1)]
+
+        def layer_norm_step(s):
+            late = s - NORM_LAG
+            if s < len(units):
+                add_bias(*units[s])
+            if 0 <= late < len(units):
+                invert(*units[late])
+            if s < len(units):
+                deviation(*units[s])
+            if 0 <= late < len(units):
+                normalise(*units[late])
+
+        factors = {}
+
+        def gate_bank(quarter, c):
+            if not 0 <= quarter < GROUPS * 4:
+                return
+            grp, g, first_t = quarter // 4, (quarter % 4) // 2, 2 * (quarter % 2)
+            if first_t == 0 and c == 0:
+                factors[(grp, g)] = [
+                    stage.tile([P, PACK, GROUP * P], F32, name="factor_%d" % b) for b in range(2)
+                ]
+            turn_and_scale(grp, factors[(grp, g)][c % 2], (1, 3)[c % 2], g, first_t + c // 2)
 
         quantise_x(0, turn_x(0))
-        spread_u1_b()
-        rows = {1: [], 3: []}
-        factors = {}
-        waiting = None
-        for r in range(GROUPS + 2):
-            for j in range(GROUP):
-                if r < GROUPS:
-                    i = r * GROUP + j
-                    unit = start_branch3(i)
-                    rows[3].append(unit[0])
-                    if waiting is not None:
-                        finish_norm(*waiting)
-                    waiting = unit
-                    if i + 1 < TOKEN_TILES:
-                        grouped = turn_x(i + 1)
-                    unit = start_branch1(i)
-                    rows[1].append(unit[0])
-                    finish_norm(*waiting)
-                    waiting = unit
-                    if i + 1 < TOKEN_TILES:
-                        quantise_x(i + 1, grouped)
-                elif waiting is not None:
-                    finish_norm(*waiting)
-                    waiting = None
-                if 1 <= r <= GROUPS:
-                    grp = r - 1
-                    if r == 1 and j == 0:
-                        gains_and_shifts()
-                    g = j // 2
-                    if j % 2 == 0:
-                        factors[(grp, g)] = [
-                            stage.tile([P, PACK, GROUP * P], F32, name="factor_%d" % b) for b in range(2)
-                        ]
-                    if j == 2:
-                        multiply(grp, 0, factors[(grp, 0)])
-                    for t in (2 * (j % 2), 2 * (j % 2) + 1):
-                        for b, branch in enumerate((1, 3)):
-                            turn_and_scale(
-                                rows[branch][grp * GROUP : (grp + 1) * GROUP], factors[(grp, g)][b], b, g, t
-                            )
-                if r >= 2:
-                    grp = r - 2
-                    if j == 0:
-                        multiply(grp, 1, factors[(grp, 1)])
-                    project(grp, j)
+        for k in range(PROJECT_LAG + TOKEN_TILES):
+            quarter = k - GATE_LAG
+            gate_bank(quarter, 0)
+            layer_norm_step(2 * k)
+            gate_bank(quarter, 1)
+            if k + 1 < TOKEN_TILES:
+                grouped = turn_x(k + 1)
+            gate_bank(quarter, 2)
+            layer_norm_step(2 * k + 1)
+            gate_bank(quarter, 3)
+            if k + 1 < TOKEN_TILES:
+                quantise_x(k + 1, grouped)
+            if k == GATE_LAG - 1:
+                gains_and_shifts()
+                spread_bias(2, c_b, "q (t p) -> q t p")
+            done = quarter - 1
+            if 0 <= done < GROUPS * 4 and done % 2 == 1:
+                multiply(done // 4, (done % 4) // 2, factors[(done // 4, (done % 4) // 2)])
+            if k >= PROJECT_LAG:
+                project((k - PROJECT_LAG) // GROUP, (k - PROJECT_LAG) % GROUP)

@@ -268,7 +268,7 @@ def tile_polymlp_skiplora_pa_kernel(
         def normalise(branch, i):
             sums, neg_mean, sum_sq, std, rstd = stats[(branch, i)]
             flat = rows[(branch, i)][:].rearrange("q g t p -> q (g t p)")
-            nc.vector.tensor_scalar(
+            nc.gpsimd.tensor_scalar(
                 out=flat, in0=flat, scalar1=neg_mean[:, 0:1], scalar2=rstd[:, 0:1],
                 op0=ALU.add, op1=ALU.mult,
             )

@@ -25,11 +25,13 @@ EPS = 1e-6
 
 TOKEN_TILES = TOKENS // P
 PASSES = DH // K_PASS
-GROUP = 4
+GROUP = 2
 GROUPS = TOKEN_TILES // GROUP
+GATE_BANKS = GROUPS * PASSES * PACK * 2
+BANKS_PER_SLOT = GATE_BANKS // TOKEN_TILES
 NORM_LAG = 2
 GATE_LAG = GROUP + 1
-PROJECT_LAG = GATE_LAG + 4
+PROJECT_LAG = GATE_LAG + GROUP
 
 FLOPS = 2 * TOKENS * (D * DH + DQ * DH + DH * D)
 
@@ -63,8 +65,6 @@ def tile_polymlp_skiplora_pa_kernel(
         stage = stack.enter_context(tc.tile_pool(name="stage", bufs=2))
         acc = stack.enter_context(tc.psum_pool(name="acc", bufs=4))
         tp = stack.enter_context(tc.psum_pool(name="tp", bufs=4))
-
-        stack.enter_context(tc.manual_schedule())
 
         bias_rows = keep.tile([P, 3, DH], BF16)
         nc.vector.memset(bias_rows[:].bitcast(I32), 0)
@@ -331,34 +331,33 @@ def tile_polymlp_skiplora_pa_kernel(
 
         factors = {}
 
-        def gate_bank(quarter, c):
-            if not 0 <= quarter < GROUPS * 4:
-                return
-            grp, g, first_t = quarter // 4, (quarter % 4) // 2, 2 * (quarter % 2)
-            if first_t == 0 and c == 0:
-                factors[(grp, g)] = [
-                    stage.tile([P, PACK, GROUP * P], F32, name="factor_%d" % b) for b in range(2)
-                ]
-            turn_and_scale(grp, factors[(grp, g)][c % 2], (1, 3)[c % 2], g, first_t + c // 2)
+        def gate_banks(first, count):
+            for index in range(max(first, 0), min(first + count, GATE_BANKS)):
+                grp, g, t, b = index // 16, (index // 8) % 2, (index // 2) % 4, index % 2
+                if t == 0 and b == 0:
+                    factors[(grp, g)] = [
+                        stage.tile([P, PACK, GROUP * P], F32, name="factor_%d" % f) for f in range(2)
+                    ]
+                turn_and_scale(grp, factors[(grp, g)][b], (1, 3)[b], g, t)
+                if t == PACK - 1 and b == 1:
+                    multiply(grp, g, factors[(grp, g)])
 
+        share = BANKS_PER_SLOT // 4
         quantise_x(0, turn_x(0))
         for k in range(PROJECT_LAG + TOKEN_TILES):
-            quarter = k - GATE_LAG
-            gate_bank(quarter, 0)
+            first = (k - GATE_LAG) * BANKS_PER_SLOT
+            gate_banks(first, share)
             layer_norm_step(2 * k)
-            gate_bank(quarter, 1)
+            gate_banks(first + share, share)
             if k + 1 < TOKEN_TILES:
                 grouped = turn_x(k + 1)
-            gate_bank(quarter, 2)
+            gate_banks(first + 2 * share, share)
             layer_norm_step(2 * k + 1)
-            gate_bank(quarter, 3)
+            gate_banks(first + 3 * share, share)
             if k + 1 < TOKEN_TILES:
                 quantise_x(k + 1, grouped)
             if k == GATE_LAG - 1:
                 gains_and_shifts()
                 spread_bias(2, c_b, "q (t p) -> q t p")
-            done = quarter - 1
-            if 0 <= done < GROUPS * 4 and done % 2 == 1:
-                multiply(done // 4, (done % 4) // 2, factors[(done // 4, (done % 4) // 2)])
             if k >= PROJECT_LAG:
                 project((k - PROJECT_LAG) // GROUP, (k - PROJECT_LAG) % GROUP)

@@ -27,11 +27,12 @@ TOKEN_TILES = TOKENS // P
 PASSES = DH // K_PASS
 GROUP = 2
 GROUPS = TOKEN_TILES // GROUP
-GATE_BANKS = GROUPS * PASSES * PACK * 2
+GATE_BANKS = GROUPS * PASSES * PACK
 BANKS_PER_SLOT = GATE_BANKS // TOKEN_TILES
 NORM_LAG = 2
 GATE_LAG = GROUP + 1
-PROJECT_LAG = GATE_LAG + GROUP
+PROJECT_LAG = TOKEN_TILES
+PROJECTS_PER_SLOT = 2
 
 FLOPS = 2 * TOKENS * (D * DH + DQ * DH + DH * D)
 
@@ -66,13 +67,14 @@ def tile_polymlp_skiplora_pa_kernel(
         acc = stack.enter_context(tc.psum_pool(name="acc", bufs=4))
         tp = stack.enter_context(tc.psum_pool(name="tp", bufs=4))
 
-        bias_rows = keep.tile([P, 3, DH], BF16)
-        nc.vector.memset(bias_rows[:].bitcast(I32), 0)
-        for v, vector in enumerate((U3_b, U1_b, C_b)):
-            nc.sync.dma_start(out=bias_rows[0:1, v, :], in_=vector.rearrange("(o n) -> o n", o=1))
-
         planes = keep.tile([P, D], U8, align_bytes=64)
         nc.vector.memset(planes[:].bitcast(I32), 0)
+
+        bias_rows = keep.tile([P, 3, DH], BF16)
+        nc.vector.memset(bias_rows[:].bitcast(I32), 0)
+
+        def load_bias_row(queue, v, vector):
+            queue.dma_start(out=bias_rows[0:1, v, :], in_=vector.rearrange("(o n) -> o n", o=1))
 
         def load_scales(scales_dram, first_plane):
             for quadrant in range(4):
@@ -97,11 +99,13 @@ def tile_polymlp_skiplora_pa_kernel(
             nc.sync.dma_start(out=x_sb[:, i, :], in_=x_rows[i * P : (i + 1) * P, :])
 
         z2_sb = keep.tile([P, TOKEN_TILES, DQ], BF16)
-        nc.sync.dma_start(out=z2_sb[:], in_=z2_rows.rearrange("(i p) d -> p i d", p=P))
+        nc.scalar.dma_start(out=z2_sb[:], in_=z2_rows.rearrange("(i p) d -> p i d", p=P))
         u3_sb = keep.tile([P, PASSES, PACK, DQ], BF16)
-        nc.sync.dma_start(
+        nc.scalar.dma_start(
             out=u3_sb[:], in_=U3_w.rearrange("(g p t) d -> p g t d", g=PASSES, t=PACK)
         )
+        load_bias_row(nc.scalar, 0, U3_b)
+        load_bias_row(nc.scalar, 1, U1_b)
         load_scales(U1_w_scales, 0)
         load_x(0)
         w1_words = load_words(U1_w_words, "w1_words")
@@ -113,6 +117,7 @@ def tile_polymlp_skiplora_pa_kernel(
                 out=ln_raw[:, v, 0 : PASSES * PACK].rearrange("p (g t) -> p g t", g=PASSES),
                 in_=vector.rearrange("(g p t) -> p g t", g=PASSES, t=PACK),
             )
+        load_bias_row(nc.sync, 2, C_b)
         alpha_raw = keep.tile([P, 1], BF16)
         nc.sync.dma_start(out=alpha_raw[:], in_=alpha.partition_broadcast(P))
         for i in range(GROUP, TOKEN_TILES):
@@ -273,18 +278,21 @@ def tile_polymlp_skiplora_pa_kernel(
                 op0=ALU.add, op1=ALU.mult,
             )
 
-        def turn_and_scale(grp, factor, branch, g, t):
-            turned = tp.tile([P, GROUP * P], F32, name="turned", tag="tp")
-            for j in range(GROUP):
-                nc.tensor.transpose(
-                    turned[:, j * P : (j + 1) * P], rows[(branch, grp * GROUP + j)][:, g, t, :], ident_f32[:]
-                )
+        def turn_and_scale(grp, factors, g, t):
+            turned = tp.tile([P, 2, GROUP * P], F32, name="turned", tag="tp")
+            for b, branch in enumerate((1, 3)):
+                for j in range(GROUP):
+                    nc.tensor.transpose(
+                        turned[:, b, j * P : (j + 1) * P], rows[(branch, grp * GROUP + j)][:, g, t, :],
+                        ident_f32[:],
+                    )
             column = g * PACK + t
-            nc.scalar.activation(
-                out=factor[:, t, :], in_=turned[:], func=ACT.Identity,
-                scale=affine[:, branch - 1, column : column + 1],
-                bias=affine[:, branch, column : column + 1],
-            )
+            for b in range(2):
+                nc.scalar.activation(
+                    out=factors[b][:, t, :], in_=turned[:, b, :], func=ACT.Identity,
+                    scale=affine[:, 2 * b, column : column + 1],
+                    bias=affine[:, 2 * b + 1, column : column + 1],
+                )
 
         def multiply(grp, g, factors):
             grouped = stage.tile([P, GROUP * P, PACK], BF16, align_bytes=64, name="h_grouped")
@@ -333,18 +341,18 @@ def tile_polymlp_skiplora_pa_kernel(
 
         def gate_banks(first, count):
             for index in range(max(first, 0), min(first + count, GATE_BANKS)):
-                grp, g, t, b = index // 16, (index // 8) % 2, (index // 2) % 4, index % 2
-                if t == 0 and b == 0:
+                grp, g, t = index // (PASSES * PACK), (index // PACK) % PASSES, index % PACK
+                if t == 0:
                     factors[(grp, g)] = [
                         stage.tile([P, PACK, GROUP * P], F32, name="factor_%d" % f) for f in range(2)
                     ]
-                turn_and_scale(grp, factors[(grp, g)][b], (1, 3)[b], g, t)
-                if t == PACK - 1 and b == 1:
+                turn_and_scale(grp, factors[(grp, g)], g, t)
+                if t == PACK - 1:
                     multiply(grp, g, factors[(grp, g)])
 
         share = BANKS_PER_SLOT // 4
         quantise_x(0, turn_x(0))
-        for k in range(PROJECT_LAG + TOKEN_TILES):
+        for k in range(PROJECT_LAG + TOKEN_TILES // PROJECTS_PER_SLOT):
             first = (k - GATE_LAG) * BANKS_PER_SLOT
             gate_banks(first, share)
             layer_norm_step(2 * k)
@@ -360,4 +368,5 @@ def tile_polymlp_skiplora_pa_kernel(
                 gains_and_shifts()
                 spread_bias(2, c_b, "q (t p) -> q t p")
             if k >= PROJECT_LAG:
-                project((k - PROJECT_LAG) // GROUP, (k - PROJECT_LAG) % GROUP)
+                for i in range((k - PROJECT_LAG) * PROJECTS_PER_SLOT, (k - PROJECT_LAG + 1) * PROJECTS_PER_SLOT):
+                    project(i // GROUP, i % GROUP)

@@ -278,7 +278,7 @@ def tile_polymlp_skiplora_pa_kernel(
                 op0=ALU.add, op1=ALU.mult,
             )
 
-        def turn_and_scale(grp, factors, g, t):
+        def turn_and_scale(grp, factors, g, t, on_vector):
             turned = tp.tile([P, 2, GROUP * P], F32, name="turned", tag="tp")
             for b, branch in enumerate((1, 3)):
                 for j in range(GROUP):
@@ -288,11 +288,18 @@ def tile_polymlp_skiplora_pa_kernel(
                     )
             column = g * PACK + t
             for b in range(2):
-                nc.scalar.activation(
-                    out=factors[b][:, t, :], in_=turned[:, b, :], func=ACT.Identity,
-                    scale=affine[:, 2 * b, column : column + 1],
-                    bias=affine[:, 2 * b + 1, column : column + 1],
-                )
+                gain = affine[:, 2 * b, column : column + 1]
+                shift = affine[:, 2 * b + 1, column : column + 1]
+                if on_vector:
+                    nc.vector.tensor_scalar(
+                        out=factors[b][:, t, :], in0=turned[:, b, :], scalar1=gain, scalar2=shift,
+                        op0=ALU.mult, op1=ALU.add,
+                    )
+                else:
+                    nc.scalar.activation(
+                        out=factors[b][:, t, :], in_=turned[:, b, :], func=ACT.Identity,
+                        scale=gain, bias=shift,
+                    )
 
         def multiply(grp, g, factors):
             grouped = stage.tile([P, GROUP * P, PACK], BF16, align_bytes=64, name="h_grouped")
@@ -339,14 +346,14 @@ def tile_polymlp_skiplora_pa_kernel(
 
         factors = {}
 
-        def gate_banks(first, count):
+        def gate_banks(first, count, vector_helps):
             for index in range(max(first, 0), min(first + count, GATE_BANKS)):
                 grp, g, t = index // (PASSES * PACK), (index // PACK) % PASSES, index % PACK
                 if t == 0:
                     factors[(grp, g)] = [
                         stage.tile([P, PACK, GROUP * P], F32, name="factor_%d" % f) for f in range(2)
                     ]
-                turn_and_scale(grp, factors[(grp, g)], g, t)
+                turn_and_scale(grp, factors[(grp, g)], g, t, vector_helps and t == PACK - 1)
                 if t == PACK - 1:
                     multiply(grp, g, factors[(grp, g)])
 
@@ -354,14 +361,15 @@ def tile_polymlp_skiplora_pa_kernel(
         quantise_x(0, turn_x(0))
         for k in range(PROJECT_LAG + TOKEN_TILES // PROJECTS_PER_SLOT):
             first = (k - GATE_LAG) * BANKS_PER_SLOT
-            gate_banks(first, share)
+            helps = k < TOKEN_TILES
+            gate_banks(first, share, helps)
             layer_norm_step(2 * k)
-            gate_banks(first + share, share)
+            gate_banks(first + share, share, helps)
             if k + 1 < TOKEN_TILES:
                 grouped = turn_x(k + 1)
-            gate_banks(first + 2 * share, share)
+            gate_banks(first + 2 * share, share, helps)
             layer_norm_step(2 * k + 1)
-            gate_banks(first + 3 * share, share)
+            gate_banks(first + 3 * share, share, helps)
             if k + 1 < TOKEN_TILES:
                 quantise_x(k + 1, grouped)
             if k == GATE_LAG - 1:

@@ -16,6 +16,7 @@ P = 128
 PACK = 4
 K_PASS = P * PACK
 BANK = 512
+QUADRANTS = 4
 
 TOKENS = 1024
 D = 1024
@@ -25,10 +26,12 @@ EPS = 1e-6
 
 TOKEN_TILES = TOKENS // P
 PASSES = DH // K_PASS
+BANKS = DH // BANK
 GROUP = 2
 GROUPS = TOKEN_TILES // GROUP
 GATE_BANKS = GROUPS * PASSES * PACK
 BANKS_PER_SLOT = GATE_BANKS // TOKEN_TILES
+
 NORM_LAG = 2
 GATE_LAG = GROUP + 1
 PROJECT_LAG = TOKEN_TILES
@@ -63,9 +66,10 @@ def tile_polymlp_skiplora_pa_kernel(
 
     with ExitStack() as stack:
         keep = stack.enter_context(tc.tile_pool(name="keep", bufs=1))
-        stage = stack.enter_context(tc.tile_pool(name="stage", bufs=2))
+        stage = stack.enter_context(tc.tile_pool(name="stage", bufs=3))
         acc = stack.enter_context(tc.psum_pool(name="acc", bufs=4))
         tp = stack.enter_context(tc.psum_pool(name="tp", bufs=4))
+
 
         planes = keep.tile([P, D], U8, align_bytes=64)
         nc.vector.memset(planes[:].bitcast(I32), 0)
@@ -77,7 +81,7 @@ def tile_polymlp_skiplora_pa_kernel(
             queue.dma_start(out=bias_rows[0:1, v, :], in_=vector.rearrange("(o n) -> o n", o=1))
 
         def load_scales(scales_dram, first_plane):
-            for quadrant in range(4):
+            for quadrant in range(QUADRANTS):
                 first_row = 32 * quadrant + 4 * first_plane
                 nc.sync.dma_start(
                     out=planes[first_row : first_row + 4 * PASSES, :].bitcast(I32),
@@ -135,7 +139,7 @@ def tile_polymlp_skiplora_pa_kernel(
         nc.vector.memset(eps[:], EPS)
 
         def spread_bias(v, spread, pattern):
-            for n in range(2):
+            for n in range(BANKS):
                 bank = acc.tile([P, BANK], F32, name="bias_bank", tag="acc")
                 nc.tensor.matmul(
                     out=bank[:], lhsT=ones[:], rhs=bias_rows[:, v, BANK * n : BANK * (n + 1)],
@@ -162,7 +166,7 @@ def tile_polymlp_skiplora_pa_kernel(
         spread_bias(0, u3_b, "q (p t) -> q t p")
         u1_b = keep.tile([P, PASSES, PACK, P], F32)
         spread_bias(1, u1_b, "q (p t) -> q t p")
-        c_b = keep.tile([P, 2, PACK, P], F32)
+        c_b = keep.tile([P, BANKS, PACK, P], F32)
 
         affine = keep.tile([P, 4, PASSES * PACK], F32)
 
@@ -194,22 +198,22 @@ def tile_polymlp_skiplora_pa_kernel(
                     nc.tensor.transpose(
                         xT[:, g, u, :], words[:, first : (K_PASS // 2) * (g + 1) : 2], ident_f32[:]
                     )
-            grouped = stage.tile([P, PASSES, P, PACK], BF16, align_bytes=64, name="x_grouped")
-            nc.scalar.copy(out=grouped[:].bitcast(F32), in_=xT[:].rearrange("p g u w -> p g w u"))
-            return grouped
+            x_grouped = stage.tile([P, PASSES, P, PACK], BF16, align_bytes=64, name="x_grouped")
+            nc.scalar.copy(out=x_grouped[:].bitcast(F32), in_=xT[:].rearrange("p g u w -> p g w u"))
+            return x_grouped
 
-        def quantise_x(i, grouped):
+        def quantise_x(i, x_grouped):
             nc.vector.quantize_mx(
                 out=x_codes[:, i].rearrange("p g w -> p (g w)").bitcast(FP8X4),
                 scales=x_scales[:, i].rearrange("p g w -> p (g w)"),
-                in_=grouped[:].rearrange("p g w t -> p (g w t)"),
+                in_=x_grouped[:].rearrange("p g w t -> p (g w t)"),
             )
 
         def mx_product(codes, scales, weight_words, first_plane, name):
-            banks = [acc.tile([P, BANK], F32, name="%s_%d" % (name, n), tag="acc") for n in range(2)]
+            banks = [acc.tile([P, BANK], F32, name="%s_%d" % (name, n), tag="acc") for n in range(BANKS)]
             for g in range(PASSES):
                 plane_row = 4 * (first_plane + g)
-                for n in range(2):
+                for n in range(BANKS):
                     nc.tensor.matmul_mx(
                         out=banks[n][:],
                         lhsT=codes[:, g, :].bitcast(FP8X4),
@@ -302,9 +306,9 @@ def tile_polymlp_skiplora_pa_kernel(
                     )
 
         def multiply(grp, g, factors):
-            grouped = stage.tile([P, GROUP * P, PACK], BF16, align_bytes=64, name="h_grouped")
+            h_grouped = stage.tile([P, GROUP * P, PACK], BF16, align_bytes=64, name="h_grouped")
             nc.vector.tensor_tensor(
-                out=grouped[:].rearrange("p (c i) t -> p c t i", i=4),
+                out=h_grouped[:].rearrange("p (c i) t -> p c t i", i=4),
                 in0=factors[0][:].rearrange("p t (c i) -> p c t i", i=4),
                 in1=factors[1][:].rearrange("p t (c i) -> p c t i", i=4),
                 op=ALU.mult,
@@ -312,7 +316,7 @@ def tile_polymlp_skiplora_pa_kernel(
             nc.vector.quantize_mx(
                 out=h_codes[:, grp, g, :].bitcast(FP8X4),
                 scales=h_scales[:, grp, g, :],
-                in_=grouped[:].rearrange("p w t -> p (w t)"),
+                in_=h_grouped[:].rearrange("p w t -> p (w t)"),
             )
 
         def project(grp, j):
@@ -320,8 +324,8 @@ def tile_polymlp_skiplora_pa_kernel(
             banks = mx_product(
                 h_codes[:, grp, :, tokens], h_scales[:, grp, :, tokens], c_words, PASSES, "y2"
             )
-            result = stage.tile([P, 2, BANK], F32, name="result", bufs=3)
-            for n in range(2):
+            result = stage.tile([P, BANKS, BANK], F32, name="result", bufs=4)
+            for n in range(BANKS):
                 nc.vector.tensor_tensor(
                     out=result[:, n, :], in0=banks[n][:],
                     in1=c_b[:, n].rearrange("q t p -> q (t p)"), op=ALU.add,
@@ -351,7 +355,7 @@ def tile_polymlp_skiplora_pa_kernel(
                 grp, g, t = index // (PASSES * PACK), (index // PACK) % PASSES, index % PACK
                 if t == 0:
                     factors[(grp, g)] = [
-                        stage.tile([P, PACK, GROUP * P], F32, name="factor_%d" % f) for f in range(2)
+                        stage.tile([P, PACK, GROUP * P], F32, name="factor_%d" % b) for b in range(2)
                     ]
                 turn_and_scale(grp, factors[(grp, g)], g, t, vector_helps and t == PACK - 1)
                 if t == PACK - 1:
@@ -366,12 +370,12 @@ def tile_polymlp_skiplora_pa_kernel(
             layer_norm_step(2 * k)
             gate_banks(first + share, share, helps)
             if k + 1 < TOKEN_TILES:
-                grouped = turn_x(k + 1)
+                x_grouped = turn_x(k + 1)
             gate_banks(first + 2 * share, share, helps)
             layer_norm_step(2 * k + 1)
             gate_banks(first + 3 * share, share, helps)
             if k + 1 < TOKEN_TILES:
-                quantise_x(k + 1, grouped)
+                quantise_x(k + 1, x_grouped)
             if k == GATE_LAG - 1:
                 gains_and_shifts()
                 spread_bias(2, c_b, "q (t p) -> q t p")

@@ -267,12 +267,12 @@ def tile_polymlp_skiplora_pa_kernel(
                 func=ACT.Square, bias=neg_mean[:, 0:1], scale=1.0, accum_out=sum_sq[:, 0:1],
             )
             nc.scalar.activation(
-                out=std[:], in_=sum_sq[:], func=ACT.Sqrt, bias=eps[:, 0:1], scale=1.0 / DH
+                out=rstd[:], in_=sum_sq[:], func=ACT.Abs_reciprocal_sqrt, bias=eps[:, 0:1], scale=1.0 / DH
             )
 
         def invert(branch, i):
             sums, neg_mean, sum_sq, std, rstd = stats[(branch, i)]
-            nc.vector.reciprocal(out=rstd[:], in_=std[:])
+            return
 
         def normalise(branch, i):
             sums, neg_mean, sum_sq, std, rstd = stats[(branch, i)]

@@ -236,17 +236,21 @@ def tile_polymlp_skiplora_pa_kernel(
                 )
             return banks
 
+        products = {}
         rows = {}
         stats = {}
 
+        def product(branch, i):
+            products[(branch, i)] = branch_product(branch, i)
+
         def add_bias(branch, i):
-            banks = branch_product(branch, i)
+            banks = products[(branch, i)]
             pattern = "q (p t) -> q t p" if branch == 1 else "q (t p) -> q t p"
             bias = u1_b if branch == 1 else u3_b
             rows[(branch, i)] = keep.tile([P, PASSES, PACK, P], F32, name="rows_%d_%d" % (branch, i))
             stats[(branch, i)] = [
                 stage.tile([P, width], F32, name=name, bufs=6)
-                for name, width in (("sums", PASSES), ("neg_mean", 1), ("sum_sq", 1), ("std", 1), ("rstd", 1))
+                for name, width in (("sums", PASSES), ("neg_mean", 1), ("sum_sq", 1), ("rstd", 1))
             ]
             sums = stats[(branch, i)][0]
             for g in range(PASSES):
@@ -255,12 +259,15 @@ def tile_polymlp_skiplora_pa_kernel(
                     in1=bias[:, g], op0=ALU.mult, op1=ALU.add, accum_out=sums[:, g : g + 1],
                 )
 
-        def deviation(branch, i):
-            sums, neg_mean, sum_sq, std, rstd = stats[(branch, i)]
+        def mean(branch, i):
+            sums, neg_mean, sum_sq, rstd = stats[(branch, i)]
             nc.vector.tensor_scalar(
                 out=neg_mean[:], in0=sums[:, 0:1], scalar1=sums[:, 1:2], scalar2=-1.0 / DH,
                 op0=ALU.add, op1=ALU.mult,
             )
+
+        def deviation(branch, i):
+            sums, neg_mean, sum_sq, rstd = stats[(branch, i)]
             squares = stage.tile([P, DH], BF16, name="squares", bufs=4)
             nc.scalar.activation(
                 out=squares[:], in_=rows[(branch, i)][:].rearrange("q g t p -> q (g t p)"),
@@ -270,19 +277,25 @@ def tile_polymlp_skiplora_pa_kernel(
                 out=rstd[:], in_=sum_sq[:], func=ACT.Abs_reciprocal_sqrt, bias=eps[:, 0:1], scale=1.0 / DH
             )
 
-        def invert(branch, i):
-            sums, neg_mean, sum_sq, std, rstd = stats[(branch, i)]
-            return
-
         def normalise(branch, i):
-            sums, neg_mean, sum_sq, std, rstd = stats[(branch, i)]
+            sums, neg_mean, sum_sq, rstd = stats[(branch, i)]
             flat = rows[(branch, i)][:].rearrange("q g t p -> q (g t p)")
             nc.gpsimd.tensor_scalar(
                 out=flat, in0=flat, scalar1=neg_mean[:, 0:1], scalar2=rstd[:, 0:1],
                 op0=ALU.add, op1=ALU.mult,
             )
 
-        def turn_and_scale(grp, factors, g, t, on_vector):
+        turned_banks = {}
+        factors = {}
+        h_tiles = {}
+
+        def place(index):
+            return index // (PASSES * PACK), (index // PACK) % PASSES, index % PACK
+
+        def turn(index):
+            if not 0 <= index < GATE_BANKS:
+                return
+            grp, g, t = place(index)
             turned = tp.tile([P, 2, GROUP * P], F32, name="turned", tag="tp")
             for b, branch in enumerate((1, 3)):
                 for j in range(GROUP):
@@ -290,95 +303,123 @@ def tile_polymlp_skiplora_pa_kernel(
                         turned[:, b, j * P : (j + 1) * P], rows[(branch, grp * GROUP + j)][:, g, t, :],
                         ident_f32[:],
                     )
+            turned_banks[index] = turned
+
+        def scale(index, vector_helps):
+            if not 0 <= index < GATE_BANKS:
+                return
+            grp, g, t = place(index)
+            if t == 0:
+                factors[(grp, g)] = [
+                    stage.tile([P, PACK, GROUP * P], F32, name="factor_%d" % b) for b in range(2)
+                ]
+            turned = turned_banks[index]
             column = g * PACK + t
             for b in range(2):
                 gain = affine[:, 2 * b, column : column + 1]
                 shift = affine[:, 2 * b + 1, column : column + 1]
-                if on_vector:
+                if vector_helps and t == PACK - 1:
                     nc.vector.tensor_scalar(
-                        out=factors[b][:, t, :], in0=turned[:, b, :], scalar1=gain, scalar2=shift,
+                        out=factors[(grp, g)][b][:, t, :], in0=turned[:, b, :], scalar1=gain, scalar2=shift,
                         op0=ALU.mult, op1=ALU.add,
                     )
                 else:
                     nc.scalar.activation(
-                        out=factors[b][:, t, :], in_=turned[:, b, :], func=ACT.Identity,
+                        out=factors[(grp, g)][b][:, t, :], in_=turned[:, b, :], func=ACT.Identity,
                         scale=gain, bias=shift,
                     )
 
-        def multiply(grp, g, factors):
+        def multiply(half):
+            if not 0 <= half < GROUPS * PASSES:
+                return
+            grp, g = half // PASSES, half % PASSES
             h_grouped = stage.tile([P, GROUP * P, PACK], BF16, align_bytes=64, name="h_grouped")
             nc.vector.tensor_tensor(
                 out=h_grouped[:].rearrange("p (c i) t -> p c t i", i=4),
-                in0=factors[0][:].rearrange("p t (c i) -> p c t i", i=4),
-                in1=factors[1][:].rearrange("p t (c i) -> p c t i", i=4),
+                in0=factors[(grp, g)][0][:].rearrange("p t (c i) -> p c t i", i=4),
+                in1=factors[(grp, g)][1][:].rearrange("p t (c i) -> p c t i", i=4),
                 op=ALU.mult,
             )
+            h_tiles[half] = h_grouped
+
+        def quantise_h(half):
+            if not 0 <= half < GROUPS * PASSES:
+                return
+            grp, g = half // PASSES, half % PASSES
             nc.vector.quantize_mx(
                 out=h_codes[:, grp, g, :].bitcast(FP8X4),
                 scales=h_scales[:, grp, g, :],
-                in_=h_grouped[:].rearrange("p w t -> p (w t)"),
+                in_=h_tiles[half][:].rearrange("p w t -> p (w t)"),
             )
 
-        def project(grp, j):
+        def project(i):
+            if not 0 <= i < TOKEN_TILES:
+                return
+            grp, j = i // GROUP, i % GROUP
             tokens = slice(j * P, (j + 1) * P)
-            banks = mx_product(
+            products[(2, i)] = mx_product(
                 h_codes[:, grp, :, tokens], h_scales[:, grp, :, tokens], c_words, PASSES, "y2"
             )
+
+        def store(i):
+            if not 0 <= i < TOKEN_TILES:
+                return
+            banks = products[(2, i)]
             result = stage.tile([P, BANKS, BANK], F32, name="result", bufs=4)
             for n in range(BANKS):
                 nc.vector.tensor_tensor(
                     out=result[:, n, :], in0=banks[n][:],
                     in1=c_b[:, n].rearrange("q t p -> q (t p)"), op=ALU.add,
                 )
-            i = grp * GROUP + j
             nc.sync.dma_start(
                 out=out_rows[i * P : (i + 1) * P, :], in_=result[:].rearrange("q n c -> q (n c)")
             )
 
         units = [(branch, i) for i in range(TOKEN_TILES) for branch in (3, 1)]
-
-        def layer_norm_step(s):
-            late = s - NORM_LAG
-            if s < len(units):
+        UNITS = len(units)
+        GATE_TICK = 6
+        counts = {"ready": 0, "projected": 0, "stored": 0}
+        x_tiles = {}
+        x_tiles[0] = turn_x(0)
+        quantise_x(0, x_tiles[0])
+        x_tiles[1] = turn_x(1)
+        product(*units[0])
+        last_tick = GATE_TICK + GATE_BANKS // 2 + 3
+        for s in range(last_tick + 1):
+            first = 2 * (s - GATE_TICK)
+            helps = s < UNITS
+            if s + 1 < UNITS:
+                product(*units[s + 1])
+            turn(first)
+            if s < UNITS:
                 add_bias(*units[s])
-            if 0 <= late < len(units):
-                invert(*units[late])
-            if s < len(units):
+            scale(first - 1, helps)
+            if s < UNITS:
+                mean(*units[s])
+            if first % PACK == 2:
+                quantise_h((first - 6) // PACK)
+                if (first - 6) // PACK % PASSES == PASSES - 1:
+                    counts["ready"] = ((first - 6) // PACK + 1) // PASSES * GROUP
+            turn(first + 1)
+            if s < UNITS:
                 deviation(*units[s])
-            if 0 <= late < len(units):
-                normalise(*units[late])
-
-        factors = {}
-
-        def gate_banks(first, count, vector_helps):
-            for index in range(max(first, 0), min(first + count, GATE_BANKS)):
-                grp, g, t = index // (PASSES * PACK), (index // PACK) % PASSES, index % PACK
-                if t == 0:
-                    factors[(grp, g)] = [
-                        stage.tile([P, PACK, GROUP * P], F32, name="factor_%d" % b) for b in range(2)
-                    ]
-                turn_and_scale(grp, factors[(grp, g)], g, t, vector_helps and t == PACK - 1)
-                if t == PACK - 1:
-                    multiply(grp, g, factors[(grp, g)])
-
-        share = BANKS_PER_SLOT // 4
-        quantise_x(0, turn_x(0))
-        for k in range(PROJECT_LAG + TOKEN_TILES // PROJECTS_PER_SLOT):
-            first = (k - GATE_LAG) * BANKS_PER_SLOT
-            helps = k < TOKEN_TILES
-            gate_banks(first, share, helps)
-            layer_norm_step(2 * k)
-            gate_banks(first + share, share, helps)
-            if k + 1 < TOKEN_TILES:
-                x_grouped = turn_x(k + 1)
-            gate_banks(first + 2 * share, share, helps)
-            layer_norm_step(2 * k + 1)
-            gate_banks(first + 3 * share, share, helps)
-            if k + 1 < TOKEN_TILES:
-                quantise_x(k + 1, x_grouped)
-            if k == GATE_LAG - 1:
+            scale(first, helps)
+            if 0 <= s - NORM_LAG < UNITS:
+                normalise(*units[s - NORM_LAG])
+            if first % PACK == 0:
+                multiply(first // PACK - 1)
+            if s % 2 == 0 and s // 2 + 1 < TOKEN_TILES:
+                quantise_x(s // 2 + 1, x_tiles[s // 2 + 1])
+            if s % 2 == 1 and (s + 1) // 2 + 1 < TOKEN_TILES:
+                x_tiles[(s + 1) // 2 + 1] = turn_x((s + 1) // 2 + 1)
+            if s == GATE_TICK - 2:
                 gains_and_shifts()
                 spread_bias(2, c_b, "q (t p) -> q t p")
-            if k >= PROJECT_LAG:
-                for i in range((k - PROJECT_LAG) * PROJECTS_PER_SLOT, (k - PROJECT_LAG + 1) * PROJECTS_PER_SLOT):
-                    project(i // GROUP, i % GROUP)
+            if s >= UNITS - 1:
+                for i in range(counts["stored"], counts["projected"]):
+                    store(i)
+                counts["stored"] = counts["projected"]
+                most = 1 if first + 2 < GATE_BANKS else GROUP
+                for i in range(counts["projected"], min(counts["ready"], counts["projected"] + most)):
+                    project(i)
+                    counts["projected"] = i + 1

@@ -280,7 +280,8 @@ def tile_polymlp_skiplora_pa_kernel(
         def normalise(branch, i):
             sums, neg_mean, sum_sq, rstd = stats[(branch, i)]
             flat = rows[(branch, i)][:].rearrange("q g t p -> q (g t p)")
-            nc.gpsimd.tensor_scalar(
+            engine = nc.vector if branch == 3 else nc.gpsimd
+            engine.tensor_scalar(
                 out=flat, in0=flat, scalar1=neg_mean[:, 0:1], scalar2=rstd[:, 0:1],
                 op0=ALU.add, op1=ALU.mult,
             )

@@ -335,23 +335,31 @@ def tile_polymlp_skiplora_pa_kernel(
                 return
             grp, g = half // PASSES, half % PASSES
             h_grouped = stage.tile([P, GROUP * P, PACK], BF16, align_bytes=64, name="h_grouped")
-            nc.vector.tensor_tensor(
-                out=h_grouped[:].rearrange("p (c i) t -> p c t i", i=4),
-                in0=factors[(grp, g)][0][:].rearrange("p t (c i) -> p c t i", i=4),
-                in1=factors[(grp, g)][1][:].rearrange("p t (c i) -> p c t i", i=4),
-                op=ALU.mult,
-            )
+            pieces = GROUP if half == GROUPS * PASSES - 1 else 1
+            width = GROUP * P // pieces
+            for piece in range(pieces):
+                tokens = slice(piece * width, (piece + 1) * width)
+                nc.vector.tensor_tensor(
+                    out=h_grouped[:, tokens, :].rearrange("p (c i) t -> p c t i", i=4),
+                    in0=factors[(grp, g)][0][:, :, tokens].rearrange("p t (c i) -> p c t i", i=4),
+                    in1=factors[(grp, g)][1][:, :, tokens].rearrange("p t (c i) -> p c t i", i=4),
+                    op=ALU.mult,
+                )
             h_tiles[half] = h_grouped
 
         def quantise_h(half):
             if not 0 <= half < GROUPS * PASSES:
                 return
             grp, g = half // PASSES, half % PASSES
-            nc.vector.quantize_mx(
-                out=h_codes[:, grp, g, :].bitcast(FP8X4),
-                scales=h_scales[:, grp, g, :],
-                in_=h_tiles[half][:].rearrange("p w t -> p (w t)"),
-            )
+            pieces = GROUP if half == GROUPS * PASSES - 1 else 1
+            width = GROUP * P // pieces
+            for piece in range(pieces):
+                tokens = slice(piece * width, (piece + 1) * width)
+                nc.vector.quantize_mx(
+                    out=h_codes[:, grp, g, tokens].bitcast(FP8X4),
+                    scales=h_scales[:, grp, g, tokens],
+                    in_=h_tiles[half][:, tokens, :].rearrange("p w t -> p (w t)"),
+                )
 
         def project(i):
             if not 0 <= i < TOKEN_TILES:
@@ -372,9 +380,14 @@ def tile_polymlp_skiplora_pa_kernel(
                     out=result[:, n, :], in0=banks[n][:],
                     in1=c_b[:, n].rearrange("q t p -> q (t p)"), op=ALU.add,
                 )
-            nc.sync.dma_start(
-                out=out_rows[i * P : (i + 1) * P, :], in_=result[:].rearrange("q n c -> q (n c)")
-            )
+                if i == TOKEN_TILES - 1:
+                    nc.sync.dma_start(
+                        out=out_rows[i * P : (i + 1) * P, n * BANK : (n + 1) * BANK], in_=result[:, n, :]
+                    )
+            if i < TOKEN_TILES - 1:
+                nc.sync.dma_start(
+                    out=out_rows[i * P : (i + 1) * P, :], in_=result[:].rearrange("q n c -> q (n c)")
+                )
 
         units = [(branch, i) for i in range(TOKEN_TILES) for branch in (3, 1)]
         UNITS = len(units)

@@ -67,22 +67,24 @@ def tile_polymlp_skiplora_pa_kernel(
     with ExitStack() as stack:
         keep = stack.enter_context(tc.tile_pool(name="keep", bufs=1))
         stage = stack.enter_context(tc.tile_pool(name="stage", bufs=3))
+        stack.enter_context(tc.manual_schedule())
         acc = stack.enter_context(tc.psum_pool(name="acc", bufs=4))
         tp = stack.enter_context(tc.psum_pool(name="tp", bufs=4))
 
 
-        planes = keep.tile([P, D], U8, align_bytes=64)
-        nc.vector.memset(planes[:].bitcast(I32), 0)
+        vectors = (U3_b, ln1_g, ln1_b, ln3_g, ln3_b, U1_b, C_b)
+        U3_B, LN1_G, LN1_B, LN3_G, LN3_B, U1_B, C_B = range(len(vectors))
+        vector_rows = keep.tile([P, DH], BF16)
+        nc.vector.memset(vector_rows[:].bitcast(I32), 0)
 
-        bias_rows = keep.tile([P, 3, DH], BF16)
-        nc.vector.memset(bias_rows[:].bitcast(I32), 0)
+        u1_planes = keep.tile([P, DH], U8, align_bytes=64)
+        nc.vector.memset(u1_planes[:].bitcast(I32), 0)
+        c_planes = keep.tile([P, D], U8, align_bytes=64)
+        nc.gpsimd.memset(c_planes[:].bitcast(I32), 0)
 
-        def load_bias_row(queue, v, vector):
-            queue.dma_start(out=bias_rows[0:1, v, :], in_=vector.rearrange("(o n) -> o n", o=1))
-
-        def load_scales(scales_dram, first_plane):
+        def load_scales(scales_dram, planes):
             for quadrant in range(QUADRANTS):
-                first_row = 32 * quadrant + 4 * first_plane
+                first_row = 32 * quadrant
                 nc.sync.dma_start(
                     out=planes[first_row : first_row + 4 * PASSES, :].bitcast(I32),
                     in_=scales_dram[:, 4 * quadrant : 4 * quadrant + 4, :].bitcast(I32),
@@ -108,42 +110,35 @@ def tile_polymlp_skiplora_pa_kernel(
         nc.scalar.dma_start(
             out=u3_sb[:], in_=U3_w.rearrange("(g p t) d -> p g t d", g=PASSES, t=PACK)
         )
-        load_bias_row(nc.scalar, 0, U3_b)
-        load_bias_row(nc.scalar, 1, U1_b)
-        load_scales(U1_w_scales, 0)
-        load_x(0)
-        w1_words = load_words(U1_w_words, "w1_words")
-        for i in range(1, GROUP):
-            load_x(i)
-        ln_raw = keep.tile([P, 4, 16], BF16)
-        for v, vector in enumerate((ln1_g, ln1_b, ln3_g, ln3_b)):
-            nc.sync.dma_start(
-                out=ln_raw[:, v, 0 : PASSES * PACK].rearrange("p (g t) -> p g t", g=PASSES),
-                in_=vector.rearrange("(g p t) -> p g t", g=PASSES, t=PACK),
-            )
-        load_bias_row(nc.sync, 2, C_b)
+        eps = keep.tile([P, 1], F32)
+        nc.vector.memset(eps[:], EPS)
+        first_rstd = keep.tile([P, 1], F32)
+        nc.scalar.activation(
+            out=first_rstd[:], in_=eps[:], func=ACT.Abs_reciprocal_sqrt, bias=eps[:, 0:1], scale=1.0
+        )
+        for r, vector in enumerate(vectors):
+            nc.sync.dma_start(out=vector_rows[r : r + 1, :], in_=vector.rearrange("(o n) -> o n", o=1))
         alpha_raw = keep.tile([P, 1], BF16)
         nc.sync.dma_start(out=alpha_raw[:], in_=alpha.partition_broadcast(P))
-        for i in range(GROUP, TOKEN_TILES):
+        load_scales(U1_w_scales, u1_planes)
+        load_x(0)
+        w1_words = load_words(U1_w_words, "w1_words")
+        for i in range(1, TOKEN_TILES):
             load_x(i)
-        load_scales(C_w_scales, PASSES)
+        load_scales(C_w_scales, c_planes)
         c_words = load_words(C_w_words, "c_words")
 
         ident_f32 = keep.tile([P, P], F32)
         make_identity(nc, ident_f32[:])
         ident_bf16 = keep.tile([P, P], BF16)
         make_identity(nc, ident_bf16[:])
-        ones = keep.tile([P, P], BF16)
-        nc.vector.memset(ones[:], 1.0)
-        eps = keep.tile([P, 1], F32)
-        nc.vector.memset(eps[:], EPS)
 
-        def spread_bias(v, spread, pattern):
+        def spread_row(r, spread, pattern):
             for n in range(BANKS):
-                bank = acc.tile([P, BANK], F32, name="bias_bank", tag="acc")
+                bank = acc.tile([P, BANK], F32, name="row_bank", tag="acc")
                 nc.tensor.matmul(
-                    out=bank[:], lhsT=ones[:], rhs=bias_rows[:, v, BANK * n : BANK * (n + 1)],
-                    start=True, stop=True,
+                    out=bank[:], lhsT=ident_bf16[:, r : r + 1].to_broadcast([P, P]),
+                    rhs=vector_rows[:, BANK * n : BANK * (n + 1)], start=True, stop=True,
                 )
                 if n == 0:
                     nc.vector.tensor_copy(out=spread[:, n], in_=bank[:].rearrange(pattern, t=PACK))
@@ -162,25 +157,29 @@ def tile_polymlp_skiplora_pa_kernel(
         u3T = keep.tile([P, PASSES, PACK * P], BF16)
         nc.scalar.copy(out=u3T[:], in_=u3T_ps[:].rearrange("d g t p -> d g (t p)"))
 
-        u3_b = keep.tile([P, PASSES, PACK, P], F32)
-        spread_bias(0, u3_b, "q (p t) -> q t p")
-        u1_b = keep.tile([P, PASSES, PACK, P], F32)
-        spread_bias(1, u1_b, "q (p t) -> q t p")
-        c_b = keep.tile([P, BANKS, PACK, P], F32)
+        affine = keep.tile([P, 5, PASSES * PACK], F32)
+        turned_vectors = tp.tile([P, PASSES * PACK, P], BF16, tag="tp")
+        for g in range(PASSES):
+            for t in range(PACK):
+                nc.tensor.transpose(
+                    turned_vectors[:, g * PACK + t, :],
+                    vector_rows[:, K_PASS * g + t : K_PASS * (g + 1) : PACK], ident_bf16[:],
+                )
+        nc.vector.tensor_copy(out=affine[:], in_=turned_vectors[:, :, 0:5].rearrange("p c r -> p r c"))
 
-        affine = keep.tile([P, 4, PASSES * PACK], F32)
+        u1_b = keep.tile([P, PASSES, PACK, P], F32)
+        spread_row(U1_B, u1_b, "q (p t) -> q t p")
+        c_b = keep.tile([P, BANKS, PACK, P], F32)
 
         def gains_and_shifts():
             alpha_f32 = keep.tile([P, 1], F32)
             nc.vector.tensor_copy(out=alpha_f32[:], in_=alpha_raw[:])
-            ln_cols = ln_raw[:, :, 0 : PASSES * PACK]
-            nc.vector.tensor_copy(out=affine[:, 0:2, :], in_=ln_cols[:, 0:2, :])
             nc.vector.tensor_scalar(
-                out=affine[:, 2, :], in0=ln_cols[:, 2, :], scalar1=alpha_f32[:, 0:1], scalar2=None,
-                op0=ALU.mult,
+                out=affine[:, LN3_G, :], in0=affine[:, LN3_G, :], scalar1=alpha_f32[:, 0:1], scalar2=-1.0,
+                op0=ALU.mult, op1=ALU.mult,
             )
             nc.vector.tensor_scalar(
-                out=affine[:, 3, :], in0=ln_cols[:, 3, :], scalar1=alpha_f32[:, 0:1], scalar2=1.0,
+                out=affine[:, LN3_B, :], in0=affine[:, LN3_B, :], scalar1=alpha_f32[:, 0:1], scalar2=1.0,
                 op0=ALU.mult, op1=ALU.add,
             )
 
@@ -189,30 +188,36 @@ def tile_polymlp_skiplora_pa_kernel(
         h_codes = keep.tile([P, GROUPS, PASSES, GROUP * P], U32, align_bytes=64)
         h_scales = keep.tile([P, GROUPS, PASSES, GROUP * P], U8, align_bytes=64)
 
+        x_turned = {}
+        x_grouped = {}
+
         def turn_x(i):
             words = x_sb[:, i, :].bitcast(F32)
-            xT = tp.tile([P, PASSES, 2, P], F32, tag="tp")
+            x_turned[i] = tp.tile([P, PASSES, 2, P], F32, name="xT", tag="tp")
             for g in range(PASSES):
                 for u in range(2):
                     first = (K_PASS // 2) * g + u
                     nc.tensor.transpose(
-                        xT[:, g, u, :], words[:, first : (K_PASS // 2) * (g + 1) : 2], ident_f32[:]
+                        x_turned[i][:, g, u, :], words[:, first : (K_PASS // 2) * (g + 1) : 2], ident_f32[:]
                     )
-            x_grouped = stage.tile([P, PASSES, P, PACK], BF16, align_bytes=64, name="x_grouped")
-            nc.scalar.copy(out=x_grouped[:].bitcast(F32), in_=xT[:].rearrange("p g u w -> p g w u"))
-            return x_grouped
 
-        def quantise_x(i, x_grouped):
+        def copy_x(i):
+            x_grouped[i] = stage.tile([P, PASSES, P, PACK], BF16, align_bytes=64, name="x_grouped")
+            nc.scalar.copy(
+                out=x_grouped[i][:].bitcast(F32), in_=x_turned[i][:].rearrange("p g u w -> p g w u")
+            )
+
+        def quantise_x(i):
             nc.vector.quantize_mx(
                 out=x_codes[:, i].rearrange("p g w -> p (g w)").bitcast(FP8X4),
                 scales=x_scales[:, i].rearrange("p g w -> p (g w)"),
-                in_=x_grouped[:].rearrange("p g w t -> p (g w t)"),
+                in_=x_grouped[i][:].rearrange("p g w t -> p (g w t)"),
             )
 
-        def mx_product(codes, scales, weight_words, first_plane, name):
+        def mx_product(codes, scales, weight_words, planes, name):
             banks = [acc.tile([P, BANK], F32, name="%s_%d" % (name, n), tag="acc") for n in range(BANKS)]
             for g in range(PASSES):
-                plane_row = 4 * (first_plane + g)
+                plane_row = 4 * g
                 for n in range(BANKS):
                     nc.tensor.matmul_mx(
                         out=banks[n][:],
@@ -225,15 +230,24 @@ def tile_polymlp_skiplora_pa_kernel(
                     )
             return banks
 
+        def add_transposed(bank, first, column, last):
+            nc.tensor.matmul(
+                out=bank[:, first : first + P], lhsT=column.to_broadcast([P, P]), rhs=ident_f32[:],
+                start=False, stop=last, is_transpose=True,
+            )
+
         def branch_product(branch, i):
             if branch == 1:
-                return mx_product(x_codes[:, i], x_scales[:, i], w1_words, 0, "y1")
+                return mx_product(x_codes[:, i], x_scales[:, i], w1_words, u1_planes, "y1")
             banks = [acc.tile([P, BANK], F32, name="y3_%d" % g, tag="acc") for g in range(PASSES)]
             for g in range(PASSES):
                 nc.tensor.matmul(
                     out=banks[g][:], lhsT=z2T[:, i * P : (i + 1) * P], rhs=u3T[:, g, :],
-                    start=True, stop=True,
+                    start=True, stop=False,
                 )
+                for t in range(PACK):
+                    column = g * PACK + t
+                    add_transposed(banks[g], t * P, affine[:, U3_B, column : column + 1], t == PACK - 1)
             return banks
 
         products = {}
@@ -244,9 +258,10 @@ def tile_polymlp_skiplora_pa_kernel(
             products[(branch, i)] = branch_product(branch, i)
 
         def add_bias(branch, i):
+            if branch == 3:
+                moments3(i)
+                return
             banks = products[(branch, i)]
-            pattern = "q (p t) -> q t p" if branch == 1 else "q (t p) -> q t p"
-            bias = u1_b if branch == 1 else u3_b
             rows[(branch, i)] = keep.tile([P, PASSES, PACK, P], F32, name="rows_%d_%d" % (branch, i))
             stats[(branch, i)] = [
                 stage.tile([P, width], F32, name=name, bufs=6)
@@ -255,11 +270,43 @@ def tile_polymlp_skiplora_pa_kernel(
             sums = stats[(branch, i)][0]
             for g in range(PASSES):
                 nc.vector.scalar_tensor_tensor(
-                    out=rows[(branch, i)][:, g], in0=banks[g][:].rearrange(pattern, t=PACK), scalar=1.0,
-                    in1=bias[:, g], op0=ALU.mult, op1=ALU.add, accum_out=sums[:, g : g + 1],
+                    out=rows[(branch, i)][:, g], in0=banks[g][:].rearrange("q (p t) -> q t p", t=PACK), scalar=1.0,
+                    in1=u1_b[:, g], op0=ALU.mult, op1=ALU.add, accum_out=sums[:, g : g + 1],
+                )
+
+        def moments3(i):
+            banks = products[(3, i)]
+            raw = stage.tile([P, PASSES, 6], F32, name="raw_moments", bufs=4)
+            mean_var = stage.tile([P, 2], F32, name="mean_var", bufs=4)
+            for g in range(PASSES):
+                nc.vector.bn_stats(out=raw[:, g, :], in_=banks[g][:])
+            nc.vector.bn_aggr(out=mean_var[:], in_=raw[:].rearrange("q g s -> q (g s)"))
+            stats[(3, i)] = mean_var
+
+        def scale3(i):
+            mean_var = stats[(3, i)]
+            rstd, neg_rstd, shift = [
+                stage.tile([P, 1], F32, name=name, bufs=4) for name in ("rstd3", "neg_rstd", "shift3")
+            ]
+            nc.scalar.activation(
+                out=rstd[:], in_=mean_var[:, 1:2], func=ACT.Abs_reciprocal_sqrt, bias=eps[:, 0:1], scale=1.0
+            )
+            nc.scalar.activation(out=neg_rstd[:], in_=rstd[:], func=ACT.Identity, scale=-1.0)
+            nc.scalar.activation(out=shift[:], in_=mean_var[:, 0:1], func=ACT.Identity, scale=rstd[:, 0:1])
+            stats[(3, i)] = (neg_rstd, shift)
+
+        def normalise3(i):
+            neg_rstd, shift = stats[(3, i)]
+            rows[(3, i)] = keep.tile([P, PASSES, PACK, P], F32, name="rows_3_%d" % i)
+            for g in range(PASSES):
+                nc.scalar.activation(
+                    out=rows[(3, i)][:, g].rearrange("q t p -> q (t p)"), in_=products[(3, i)][g][:],
+                    func=ACT.Identity, scale=neg_rstd[:, 0:1], bias=shift[:, 0:1],
                 )
 
         def mean(branch, i):
+            if branch == 3:
+                return
             sums, neg_mean, sum_sq, rstd = stats[(branch, i)]
             nc.vector.tensor_scalar(
                 out=neg_mean[:], in0=sums[:, 0:1], scalar1=sums[:, 1:2], scalar2=-1.0 / DH,
@@ -267,6 +314,9 @@ def tile_polymlp_skiplora_pa_kernel(
             )
 
         def deviation(branch, i):
+            if branch == 3:
+                scale3(i)
+                return
             sums, neg_mean, sum_sq, rstd = stats[(branch, i)]
             squares = stage.tile([P, DH], BF16, name="squares", bufs=4)
             nc.scalar.activation(
@@ -278,6 +328,9 @@ def tile_polymlp_skiplora_pa_kernel(
             )
 
         def normalise(branch, i):
+            if branch == 3:
+                normalise3(i)
+                return
             sums, neg_mean, sum_sq, rstd = stats[(branch, i)]
             flat = rows[(branch, i)][:].rearrange("q g t p -> q (g t p)")
             engine = nc.vector if branch == 3 else nc.gpsimd
@@ -317,8 +370,8 @@ def tile_polymlp_skiplora_pa_kernel(
             turned = turned_banks[index]
             column = g * PACK + t
             for b in range(2):
-                gain = affine[:, 2 * b, column : column + 1]
-                shift = affine[:, 2 * b + 1, column : column + 1]
+                gain = affine[:, (LN1_G, LN3_G)[b], column : column + 1]
+                shift = affine[:, (LN1_B, LN3_B)[b], column : column + 1]
                 if vector_helps and t == PACK - 1:
                     nc.vector.tensor_scalar(
                         out=factors[(grp, g)][b][:, t, :], in0=turned[:, b, :], scalar1=gain, scalar2=shift,
@@ -367,7 +420,7 @@ def tile_polymlp_skiplora_pa_kernel(
             grp, j = i // GROUP, i % GROUP
             tokens = slice(j * P, (j + 1) * P)
             products[(2, i)] = mx_product(
-                h_codes[:, grp, :, tokens], h_scales[:, grp, :, tokens], c_words, PASSES, "y2"
+                h_codes[:, grp, :, tokens], h_scales[:, grp, :, tokens], c_words, c_planes, "y2"
             )
 
         def store(i):
@@ -389,51 +442,36 @@ def tile_polymlp_skiplora_pa_kernel(
                     out=out_rows[i * P : (i + 1) * P, :], in_=result[:].rearrange("q n c -> q (n c)")
                 )
 
-        units = [(branch, i) for i in range(TOKEN_TILES) for branch in (3, 1)]
-        UNITS = len(units)
-        GATE_TICK = 6
-        counts = {"ready": 0, "projected": 0, "stored": 0}
-        x_tiles = {}
-        x_tiles[0] = turn_x(0)
-        quantise_x(0, x_tiles[0])
-        x_tiles[1] = turn_x(1)
-        product(*units[0])
-        last_tick = GATE_TICK + GATE_BANKS // 2 + 3
-        for s in range(last_tick + 1):
-            first = 2 * (s - GATE_TICK)
-            helps = s < UNITS
-            if s + 1 < UNITS:
-                product(*units[s + 1])
-            turn(first)
-            if s < UNITS:
-                add_bias(*units[s])
-            scale(first - 1, helps)
-            if s < UNITS:
-                mean(*units[s])
-            if first % PACK == 2:
-                quantise_h((first - 6) // PACK)
-                if (first - 6) // PACK % PASSES == PASSES - 1:
-                    counts["ready"] = ((first - 6) // PACK + 1) // PASSES * GROUP
-            turn(first + 1)
-            if s < UNITS:
-                deviation(*units[s])
-            scale(first, helps)
-            if 0 <= s - NORM_LAG < UNITS:
-                normalise(*units[s - NORM_LAG])
-            if first % PACK == 0:
-                multiply(first // PACK - 1)
-            if s % 2 == 0 and s // 2 + 1 < TOKEN_TILES:
-                quantise_x(s // 2 + 1, x_tiles[s // 2 + 1])
-            if s % 2 == 1 and (s + 1) // 2 + 1 < TOKEN_TILES:
-                x_tiles[(s + 1) // 2 + 1] = turn_x((s + 1) // 2 + 1)
-            if s == GATE_TICK - 2:
-                gains_and_shifts()
-                spread_bias(2, c_b, "q (t p) -> q t p")
-            if s >= UNITS - 1:
-                for i in range(counts["stored"], counts["projected"]):
-                    store(i)
-                counts["stored"] = counts["projected"]
-                most = 1 if first + 2 < GATE_BANKS else GROUP
-                for i in range(counts["projected"], min(counts["ready"], counts["projected"] + most)):
-                    project(i)
-                    counts["projected"] = i + 1
+        PACE = 4
+        lags = {
+            "gains": -36, "spread": -36, "turn_x": -2, "copy_x": -1, "quantise_x": 2,
+            "product": {3: -3, 1: 3}, "add_bias": {3: -2, 1: 4}, "mean": {3: 0, 1: 5},
+            "deviation": {3: -1, 1: 6}, "normalise": {3: 0, 1: 7},
+            "turn": 16, "scale": 18, "multiply": 22, "quantise_h": 26, "project": 32, "store": 36,
+        }
+        plan = []
+
+        def put(position, stage_function, *which):
+            plan.append((position, len(plan), stage_function, which))
+
+        for i in range(TOKEN_TILES):
+            for name, stage_function in (("turn_x", turn_x), ("copy_x", copy_x), ("quantise_x", quantise_x)):
+                put(lags[name] + PACE * i // 2, stage_function, i)
+            for branch in (3, 1):
+                for name, stage_function in (
+                    ("product", product), ("add_bias", add_bias), ("mean", mean), ("deviation", deviation), ("normalise", normalise)
+                ):
+                    put(lags[name][branch] + PACE * i, stage_function, branch, i)
+        for k in range(GATE_BANKS):
+            put(lags["turn"] + k, turn, k)
+            put(lags["scale"] + k, scale, k, k < 22)
+        for half in range(GROUPS * PASSES):
+            put(lags["multiply"] + PACE * half, multiply, half)
+            put(lags["quantise_h"] + PACE * half, quantise_h, half)
+        for i in range(TOKEN_TILES):
+            put(lags["project"] + PACE * i, project, i)
+            put(lags["store"] + PACE * i, store, i)
+        put(lags["spread"], spread_row, C_B, c_b, "q (t p) -> q t p")
+        put(lags["gains"], gains_and_shifts)
+        for position, order, stage_function, which in sorted(plan):
+            stage_function(*which)

@@ -27,15 +27,7 @@ EPS = 1e-6
 TOKEN_TILES = TOKENS // P
 PASSES = DH // K_PASS
 BANKS = DH // BANK
-GROUP = 2
-GROUPS = TOKEN_TILES // GROUP
-GATE_BANKS = GROUPS * PASSES * PACK
-BANKS_PER_SLOT = GATE_BANKS // TOKEN_TILES
-
-NORM_LAG = 2
-GATE_LAG = GROUP + 1
-PROJECT_LAG = TOKEN_TILES
-PROJECTS_PER_SLOT = 2
+PAIR = 2
 
 FLOPS = 2 * TOKENS * (D * DH + DQ * DH + DH * D)
 
@@ -60,9 +52,9 @@ def tile_polymlp_skiplora_pa_kernel(
     out,
 ):
     nc = tc.nc
-    x_rows = x.flatten_outer_dims()
-    z2_rows = z2.flatten_outer_dims()
-    out_rows = out.flatten_outer_dims()
+    x_rows = x.flatten_outer_dims().rearrange("(p i) d -> p i d", i=TOKEN_TILES)
+    z2_rows = z2.flatten_outer_dims().rearrange("(p i) d -> p i d", i=TOKEN_TILES)
+    out_rows = out.flatten_outer_dims().rearrange("(p i) d -> p i d", i=TOKEN_TILES)
 
     with ExitStack() as stack:
         keep = stack.enter_context(tc.tile_pool(name="keep", bufs=1))
@@ -102,13 +94,14 @@ def tile_polymlp_skiplora_pa_kernel(
         x_sb = keep.tile([P, TOKEN_TILES, D], BF16)
 
         def load_x(i):
-            nc.sync.dma_start(out=x_sb[:, i, :], in_=x_rows[i * P : (i + 1) * P, :])
+            nc.sync.dma_start(out=x_sb[:, i, :], in_=x_rows[:, i, :])
 
         z2_sb = keep.tile([P, TOKEN_TILES, DQ], BF16)
-        nc.scalar.dma_start(out=z2_sb[:], in_=z2_rows.rearrange("(i p) d -> p i d", p=P))
-        u3_sb = keep.tile([P, PASSES, PACK, DQ], BF16)
+        nc.scalar.dma_start(out=z2_sb[:], in_=z2_rows)
+        u3_sb = keep.tile([P, PASSES * PACK, DQ], BF16)
         nc.scalar.dma_start(
-            out=u3_sb[:], in_=U3_w.rearrange("(g p t) d -> p g t d", g=PASSES, t=PACK)
+            out=u3_sb[:].rearrange("p (g t) d -> p g t d", g=PASSES),
+            in_=U3_w.rearrange("(g p t) d -> p g t d", g=PASSES, t=PACK),
         )
         eps = keep.tile([P, 1], F32)
         nc.vector.memset(eps[:], EPS)
@@ -128,68 +121,170 @@ def tile_polymlp_skiplora_pa_kernel(
         load_scales(C_w_scales, c_planes)
         c_words = load_words(C_w_words, "c_words")
 
-        ident_f32 = keep.tile([P, P], F32)
-        make_identity(nc, ident_f32[:])
         ident_bf16 = keep.tile([P, P], BF16)
         make_identity(nc, ident_bf16[:])
+        ident_f32 = keep.tile([P, P], F32)
+        nc.vector.tensor_copy(out=ident_f32[:], in_=ident_bf16[:])
 
-        def spread_row(r, spread, pattern):
+        def spread_row(r, spread, pattern, engines):
             for n in range(BANKS):
                 bank = acc.tile([P, BANK], F32, name="row_bank", tag="acc")
                 nc.tensor.matmul(
                     out=bank[:], lhsT=ident_bf16[:, r : r + 1].to_broadcast([P, P]),
                     rhs=vector_rows[:, BANK * n : BANK * (n + 1)], start=True, stop=True,
                 )
-                if n == 0:
+                if engines[n] == "vector":
                     nc.vector.tensor_copy(out=spread[:, n], in_=bank[:].rearrange(pattern, t=PACK))
                 else:
                     nc.scalar.copy(out=spread[:, n], in_=bank[:].rearrange(pattern, t=PACK))
 
-        z2T_ps = tp.tile([P, TOKENS], BF16, tag="tp")
-        for i in range(TOKEN_TILES):
-            nc.tensor.transpose(z2T_ps[:, i * P : (i + 1) * P], z2_sb[:, i, :], ident_bf16[:])
+        u1_b = keep.tile([P, PASSES, PACK, P], F32)
+        c_b = keep.tile([P, BANKS, PACK, P], F32)
+
         z2T = keep.tile([P, TOKENS], BF16)
-        nc.vector.tensor_copy(out=z2T[:], in_=z2T_ps[:])
-        u3T_ps = tp.tile([P, PASSES, PACK, P], BF16, tag="tp")
-        for g in range(PASSES):
-            for t in range(PACK):
-                nc.tensor.transpose(u3T_ps[:, g, t, :], u3_sb[:, g, t, :], ident_bf16[:])
-        u3T = keep.tile([P, PASSES, PACK * P], BF16)
-        nc.scalar.copy(out=u3T[:], in_=u3T_ps[:].rearrange("d g t p -> d g (t p)"))
+        z2T_f32 = keep.tile([P, TOKENS], F32)
+        u3T = keep.tile([P, PASSES * PACK, P], BF16)
+
+        def turn_z2():
+            turned = tp.tile([P, TOKENS], BF16, name="z2T_ps", tag="tp")
+            for i in range(TOKEN_TILES):
+                nc.tensor.transpose(turned[:, i * P : (i + 1) * P], z2_sb[:, i, :], ident_bf16[:])
+            nc.vector.tensor_copy(out=z2T[:], in_=turned[:])
+            nc.scalar.copy(out=z2T_f32[:], in_=turned[:])
+
+        def turn_u3():
+            turned = tp.tile([P, PASSES * PACK, P], BF16, name="u3T_ps", tag="tp")
+            for c in range(PASSES * PACK):
+                nc.tensor.transpose(turned[:, c, :], u3_sb[:, c, :], ident_bf16[:])
+            nc.scalar.copy(out=u3T[:], in_=turned[:])
 
         affine = keep.tile([P, 5, PASSES * PACK], F32)
-        turned_vectors = tp.tile([P, PASSES * PACK, P], BF16, tag="tp")
-        for g in range(PASSES):
-            for t in range(PACK):
-                nc.tensor.transpose(
-                    turned_vectors[:, g * PACK + t, :],
-                    vector_rows[:, K_PASS * g + t : K_PASS * (g + 1) : PACK], ident_bf16[:],
-                )
-        nc.vector.tensor_copy(out=affine[:], in_=turned_vectors[:, :, 0:5].rearrange("p c r -> p r c"))
 
-        u1_b = keep.tile([P, PASSES, PACK, P], F32)
-        spread_row(U1_B, u1_b, "q (p t) -> q t p")
-        c_b = keep.tile([P, BANKS, PACK, P], F32)
+        def turn_vectors():
+            turned = tp.tile([P, PASSES * PACK, P], BF16, name="vectors_ps", tag="tp")
+            for g in range(PASSES):
+                for t in range(PACK):
+                    nc.tensor.transpose(
+                        turned[:, g * PACK + t, :], vector_rows[:, K_PASS * g + t : K_PASS * (g + 1) : PACK],
+                        ident_bf16[:],
+                    )
+            nc.vector.tensor_copy(out=affine[:], in_=turned[:, :, 0:5].rearrange("p c r -> p r c"))
 
         def gains_and_shifts():
             alpha_f32 = keep.tile([P, 1], F32)
             nc.vector.tensor_copy(out=alpha_f32[:], in_=alpha_raw[:])
             nc.vector.tensor_scalar(
-                out=affine[:, LN3_G, :], in0=affine[:, LN3_G, :], scalar1=alpha_f32[:, 0:1], scalar2=-1.0,
-                op0=ALU.mult, op1=ALU.mult,
+                out=affine[:, LN3_G, :], in0=affine[:, LN3_G, :], scalar1=alpha_f32[:, 0:1], scalar2=None,
+                op0=ALU.mult,
             )
             nc.vector.tensor_scalar(
                 out=affine[:, LN3_B, :], in0=affine[:, LN3_B, :], scalar1=alpha_f32[:, 0:1], scalar2=1.0,
                 op0=ALU.mult, op1=ALU.add,
             )
 
+        b_and_one = keep.tile([P, PASSES * PACK, 2], BF16)
+        nc.gpsimd.memset(b_and_one[:], 1.0)
+        b_sums = keep.tile([P, 2], F32)
+        ones_f32 = keep.tile([P, P], F32)
+        nc.gpsimd.memset(ones_f32[:], 1.0)
+        form = keep.tile([P, DQ + 2], F32)
+        b_means = keep.tile([P, 2], F32)
+        square_eps = keep.tile([P, 1], F32)
+        quadratic = keep.tile([P, TOKEN_TILES], F32)
+        linear = keep.tile([P, TOKEN_TILES, 2], F32)
+        neg_mean3 = keep.tile([P, TOKEN_TILES], F32)
+        rstd3 = keep.tile([P, TOKEN_TILES], F32)
+        rstd3_row = keep.tile([P, TOKENS], F32)
+        gram_banks = {}
+
+        def bias_sums3():
+            column = affine[:, U3_B, :]
+            nc.vector.tensor_copy(out=b_and_one[:, :, 0], in_=column)
+            squares = stage.tile([P, PASSES * PACK], F32, name="b_squares")
+            nc.vector.reduce_sum(out=b_sums[:, 0:1], in_=column, axis=mybir.AxisListType.X)
+            nc.vector.scalar_tensor_tensor(
+                out=squares[:], in0=column, scalar=1.0, in1=column, op0=ALU.mult, op1=ALU.mult,
+                accum_out=b_sums[:, 1:2],
+            )
+
+        def gram3():
+            gram = tp.tile([P, BANK], F32, name="gram_ps", tag="tp")
+            for c in range(PASSES * PACK):
+                nc.tensor.matmul(
+                    out=gram[:, 0:DQ], lhsT=u3_sb[:, c, :], rhs=u3_sb[:, c, :],
+                    start=(c == 0), stop=(c == PASSES * PACK - 1),
+                )
+            gram_banks[0] = gram
+
+        def gram_bias3():
+            gram = gram_banks[0]
+            for c in range(PASSES * PACK):
+                nc.tensor.matmul(
+                    out=gram[:, DQ : DQ + 2], lhsT=u3_sb[:, c, :], rhs=b_and_one[:, c, :],
+                    start=(c == 0), stop=(c == PASSES * PACK - 1),
+                )
+            nc.tensor.matmul(out=gram[:, 256:258], lhsT=ones_f32[:], rhs=b_sums[:], start=True, stop=True)
+            nc.scalar.activation(
+                out=form[:], in_=gram[:, 0 : DQ + 2], func=ACT.Identity, scale=1.0 / DH
+            )
+            nc.scalar.activation(
+                out=b_means[:], in_=gram[:, 256:258], func=ACT.Identity, scale=1.0 / DH
+            )
+
+        FORM_TILES = 3
+
+        def forms3(first):
+            tiles = range(first, min(first + FORM_TILES, TOKEN_TILES))
+            bank = tp.tile([P, FORM_TILES, DQ + 2], F32, name="forms_ps", tag="tp")
+            for j, i in enumerate(tiles):
+                nc.tensor.matmul(
+                    out=bank[:, j, :], lhsT=z2T_f32[:, i * P : (i + 1) * P], rhs=form[:], start=True, stop=True
+                )
+            for j, i in enumerate(tiles):
+                z_products = stage.tile([P, DQ], F32, name="z_products")
+                nc.vector.scalar_tensor_tensor(
+                    out=z_products[:], in0=bank[:, j, 0:DQ], scalar=1.0, in1=z2_sb[:, i, :], op0=ALU.mult,
+                    op1=ALU.mult, accum_out=quadratic[:, i : i + 1],
+                )
+            nc.scalar.copy(
+                out=linear[:, first : first + len(tiles), :], in_=bank[:, 0 : len(tiles), DQ : DQ + 2]
+            )
+
+        def finish3():
+            mean_square = keep.tile([P, TOKEN_TILES], F32)
+            square_mean = keep.tile([P, TOKEN_TILES], F32)
+            variance = keep.tile([P, TOKEN_TILES], F32)
+            nc.vector.tensor_scalar(
+                out=neg_mean3[:], in0=linear[:, :, 1], scalar1=b_means[:, 0:1], scalar2=-1.0, op0=ALU.add, op1=ALU.mult
+            )
+            nc.vector.scalar_tensor_tensor(
+                out=mean_square[:], in0=linear[:, :, 0], scalar=2.0, in1=quadratic[:], op0=ALU.mult, op1=ALU.add
+            )
+            nc.vector.tensor_scalar(
+                out=square_eps[:], in0=b_means[:, 1:2], scalar1=EPS, scalar2=None, op0=ALU.add
+            )
+            nc.vector.tensor_tensor(out=square_mean[:], in0=neg_mean3[:], in1=neg_mean3[:], op=ALU.mult)
+            nc.vector.tensor_tensor(out=variance[:], in0=mean_square[:], in1=square_mean[:], op=ALU.subtract)
+            nc.scalar.activation(
+                out=rstd3[:], in_=variance[:], func=ACT.Abs_reciprocal_sqrt, bias=square_eps[:, 0:1], scale=1.0
+            )
+
+        def spread_rstd3(half):
+            spread = tp.tile([P, BANK], F32, name="rstd_ps", tag="tp")
+            for j in range(BANK // P):
+                i = half * (BANK // P) + j
+                nc.tensor.transpose(
+                    spread[:, j * P : (j + 1) * P], rstd3[:, i : i + 1].to_broadcast([P, P]), ident_f32[:]
+                )
+            nc.scalar.copy(out=rstd3_row[:, half * BANK : (half + 1) * BANK], in_=spread[:])
+
         x_codes = keep.tile([P, TOKEN_TILES, PASSES, P], U32, align_bytes=64)
         x_scales = keep.tile([P, TOKEN_TILES, PASSES, P], U8, align_bytes=64)
-        h_codes = keep.tile([P, GROUPS, PASSES, GROUP * P], U32, align_bytes=64)
-        h_scales = keep.tile([P, GROUPS, PASSES, GROUP * P], U8, align_bytes=64)
+        h_codes = keep.tile([P, TOKEN_TILES, PASSES, P], U32, align_bytes=64)
+        h_scales = keep.tile([P, TOKEN_TILES, PASSES, P], U8, align_bytes=64)
 
         x_turned = {}
-        x_grouped = {}
+        x_tiles = {}
 
         def turn_x(i):
             words = x_sb[:, i, :].bitcast(F32)
@@ -201,24 +296,24 @@ def tile_polymlp_skiplora_pa_kernel(
                         x_turned[i][:, g, u, :], words[:, first : (K_PASS // 2) * (g + 1) : 2], ident_f32[:]
                     )
 
-        def copy_x(i):
-            x_grouped[i] = stage.tile([P, PASSES, P, PACK], BF16, align_bytes=64, name="x_grouped")
+        def group_x(i):
+            x_tiles[i] = stage.tile([P, PASSES, P, PACK], BF16, align_bytes=64, name="x_grouped")
             nc.scalar.copy(
-                out=x_grouped[i][:].bitcast(F32), in_=x_turned[i][:].rearrange("p g u w -> p g w u")
+                out=x_tiles[i][:].bitcast(F32), in_=x_turned[i][:].rearrange("p g u w -> p g w u")
             )
 
         def quantise_x(i):
             nc.vector.quantize_mx(
                 out=x_codes[:, i].rearrange("p g w -> p (g w)").bitcast(FP8X4),
                 scales=x_scales[:, i].rearrange("p g w -> p (g w)"),
-                in_=x_grouped[i][:].rearrange("p g w t -> p (g w t)"),
+                in_=x_tiles[i][:].rearrange("p g w t -> p (g w t)"),
             )
 
         def mx_product(codes, scales, weight_words, planes, name):
             banks = [acc.tile([P, BANK], F32, name="%s_%d" % (name, n), tag="acc") for n in range(BANKS)]
-            for g in range(PASSES):
-                plane_row = 4 * g
-                for n in range(BANKS):
+            for n in range(BANKS):
+                for g in range(PASSES):
+                    plane_row = 4 * g
                     nc.tensor.matmul_mx(
                         out=banks[n][:],
                         lhsT=codes[:, g, :].bitcast(FP8X4),
@@ -236,196 +331,124 @@ def tile_polymlp_skiplora_pa_kernel(
                 start=False, stop=last, is_transpose=True,
             )
 
-        def branch_product(branch, i):
-            if branch == 1:
-                return mx_product(x_codes[:, i], x_scales[:, i], w1_words, u1_planes, "y1")
-            banks = [acc.tile([P, BANK], F32, name="y3_%d" % g, tag="acc") for g in range(PASSES)]
-            for g in range(PASSES):
-                nc.tensor.matmul(
-                    out=banks[g][:], lhsT=z2T[:, i * P : (i + 1) * P], rhs=u3T[:, g, :],
-                    start=True, stop=False,
-                )
-                for t in range(PACK):
-                    column = g * PACK + t
-                    add_transposed(banks[g], t * P, affine[:, U3_B, column : column + 1], t == PACK - 1)
-            return banks
-
-        products = {}
         rows = {}
+        products = {}
         stats = {}
 
-        def product(branch, i):
-            products[(branch, i)] = branch_product(branch, i)
+        gate3 = keep.tile([P, PASSES * PACK, TOKENS], F32)
+        turned_banks = {}
 
-        def add_bias(branch, i):
-            if branch == 3:
-                moments3(i)
-                return
-            banks = products[(branch, i)]
-            rows[(branch, i)] = keep.tile([P, PASSES, PACK, P], F32, name="rows_%d_%d" % (branch, i))
-            stats[(branch, i)] = [
-                stage.tile([P, width], F32, name=name, bufs=6)
-                for name, width in (("sums", PASSES), ("neg_mean", 1), ("sum_sq", 1), ("rstd", 1))
-            ]
-            sums = stats[(branch, i)][0]
+        def product3(c, half):
+            bank = tp.tile([P, BANK], F32, name="y3", tag="tp")
+            nc.tensor.matmul(
+                out=bank[:], lhsT=u3T[:, c, :], rhs=z2T[:, half * BANK : (half + 1) * BANK], start=True, stop=False
+            )
+            tiles = BANK // P
+            for j in range(tiles):
+                i = half * tiles + j
+                add_transposed(bank, j * P, neg_mean3[:, i : i + 1], j == tiles - 1)
+            turned_banks[(3, c, half)] = bank
+
+        normal3 = {}
+
+        def normalise3(c, half):
+            normal3[(c, half)] = stage.tile([P, BANK], F32, name="normal3")
+            row = rstd3_row[:, half * BANK : (half + 1) * BANK]
+            nc.vector.scalar_tensor_tensor(
+                out=normal3[(c, half)][:], in0=turned_banks[(3, c, half)][:], scalar=affine[:, U3_B, c : c + 1],
+                in1=row, op0=ALU.add, op1=ALU.mult,
+            )
+
+        def gain3(c, half):
+            nc.scalar.activation(
+                out=gate3[:, c, half * BANK : (half + 1) * BANK], in_=normal3[(c, half)][:], func=ACT.Identity,
+                scale=affine[:, LN3_G, c : c + 1], bias=affine[:, LN3_B, c : c + 1],
+            )
+
+        def product1(i):
+            products[(1, i)] = mx_product(x_codes[:, i], x_scales[:, i], w1_words, u1_planes, "y1")
+
+        def add_bias1(i):
+            rows[(1, i)] = keep.tile([P, PASSES, PACK, P], F32, name="rows1_%d" % i)
+            sums = stage.tile([P, PASSES], F32, name="sums", bufs=4)
             for g in range(PASSES):
                 nc.vector.scalar_tensor_tensor(
-                    out=rows[(branch, i)][:, g], in0=banks[g][:].rearrange("q (p t) -> q t p", t=PACK), scalar=1.0,
-                    in1=u1_b[:, g], op0=ALU.mult, op1=ALU.add, accum_out=sums[:, g : g + 1],
+                    out=rows[(1, i)][:, g], in0=products[(1, i)][g][:].rearrange("q (p t) -> q t p", t=PACK),
+                    scalar=1.0, in1=u1_b[:, g], op0=ALU.mult, op1=ALU.add, accum_out=sums[:, g : g + 1],
                 )
+            stats[(1, i)] = sums
 
-        def moments3(i):
-            banks = products[(3, i)]
-            raw = stage.tile([P, PASSES, 6], F32, name="raw_moments", bufs=4)
-            mean_var = stage.tile([P, 2], F32, name="mean_var", bufs=4)
-            for g in range(PASSES):
-                nc.vector.bn_stats(out=raw[:, g, :], in_=banks[g][:])
-            nc.vector.bn_aggr(out=mean_var[:], in_=raw[:].rearrange("q g s -> q (g s)"))
-            stats[(3, i)] = mean_var
-
-        def scale3(i):
-            mean_var = stats[(3, i)]
-            rstd, neg_rstd, shift = [
-                stage.tile([P, 1], F32, name=name, bufs=4) for name in ("rstd3", "neg_rstd", "shift3")
-            ]
-            nc.scalar.activation(
-                out=rstd[:], in_=mean_var[:, 1:2], func=ACT.Abs_reciprocal_sqrt, bias=eps[:, 0:1], scale=1.0
-            )
-            nc.scalar.activation(out=neg_rstd[:], in_=rstd[:], func=ACT.Identity, scale=-1.0)
-            nc.scalar.activation(out=shift[:], in_=mean_var[:, 0:1], func=ACT.Identity, scale=rstd[:, 0:1])
-            stats[(3, i)] = (neg_rstd, shift)
-
-        def normalise3(i):
-            neg_rstd, shift = stats[(3, i)]
-            rows[(3, i)] = keep.tile([P, PASSES, PACK, P], F32, name="rows_3_%d" % i)
-            for g in range(PASSES):
-                nc.scalar.activation(
-                    out=rows[(3, i)][:, g].rearrange("q t p -> q (t p)"), in_=products[(3, i)][g][:],
-                    func=ACT.Identity, scale=neg_rstd[:, 0:1], bias=shift[:, 0:1],
-                )
-
-        def mean(branch, i):
-            if branch == 3:
-                return
-            sums, neg_mean, sum_sq, rstd = stats[(branch, i)]
+        def mean1(i):
+            sums = stats[(1, i)]
+            neg_mean = stage.tile([P, 1], F32, name="neg_mean", bufs=4)
             nc.vector.tensor_scalar(
                 out=neg_mean[:], in0=sums[:, 0:1], scalar1=sums[:, 1:2], scalar2=-1.0 / DH,
                 op0=ALU.add, op1=ALU.mult,
             )
+            stats[(1, i)] = neg_mean
 
-        def deviation(branch, i):
-            if branch == 3:
-                scale3(i)
-                return
-            sums, neg_mean, sum_sq, rstd = stats[(branch, i)]
-            squares = stage.tile([P, DH], BF16, name="squares", bufs=4)
+        def deviation1(i):
+            neg_mean = stats[(1, i)]
+            sum_sq = stage.tile([P, 1], F32, name="sum_sq", bufs=4)
+            rstd = stage.tile([P, 1], F32, name="rstd1", bufs=4)
+            squares = stage.tile([P, DH], BF16, name="squares")
             nc.scalar.activation(
-                out=squares[:], in_=rows[(branch, i)][:].rearrange("q g t p -> q (g t p)"),
+                out=squares[:], in_=rows[(1, i)][:].rearrange("q g t p -> q (g t p)"),
                 func=ACT.Square, bias=neg_mean[:, 0:1], scale=1.0, accum_out=sum_sq[:, 0:1],
             )
             nc.scalar.activation(
                 out=rstd[:], in_=sum_sq[:], func=ACT.Abs_reciprocal_sqrt, bias=eps[:, 0:1], scale=1.0 / DH
             )
+            stats[(1, i)] = (neg_mean, rstd)
 
-        def normalise(branch, i):
-            if branch == 3:
-                normalise3(i)
-                return
-            sums, neg_mean, sum_sq, rstd = stats[(branch, i)]
-            flat = rows[(branch, i)][:].rearrange("q g t p -> q (g t p)")
-            engine = nc.vector if branch == 3 else nc.gpsimd
-            engine.tensor_scalar(
+        def normalise1(i):
+            neg_mean, rstd = stats[(1, i)]
+            flat = rows[(1, i)][:].rearrange("q g t p -> q (g t p)")
+            nc.gpsimd.tensor_scalar(
                 out=flat, in0=flat, scalar1=neg_mean[:, 0:1], scalar2=rstd[:, 0:1],
                 op0=ALU.add, op1=ALU.mult,
             )
 
-        turned_banks = {}
-        factors = {}
+        gate1 = {}
         h_tiles = {}
 
-        def place(index):
-            return index // (PASSES * PACK), (index // PACK) % PASSES, index % PACK
+        def turn1(i, g):
+            turned = tp.tile([P, PACK, P], F32, name="turned1", tag="tp")
+            for t in range(PACK):
+                nc.tensor.transpose(turned[:, t, :], rows[(1, i)][:, g, t, :], ident_f32[:])
+            turned_banks[(1, i, g)] = turned
 
-        def turn(index):
-            if not 0 <= index < GATE_BANKS:
-                return
-            grp, g, t = place(index)
-            turned = tp.tile([P, 2, GROUP * P], F32, name="turned", tag="tp")
-            for b, branch in enumerate((1, 3)):
-                for j in range(GROUP):
-                    nc.tensor.transpose(
-                        turned[:, b, j * P : (j + 1) * P], rows[(branch, grp * GROUP + j)][:, g, t, :],
-                        ident_f32[:],
-                    )
-            turned_banks[index] = turned
-
-        def scale(index, vector_helps):
-            if not 0 <= index < GATE_BANKS:
-                return
-            grp, g, t = place(index)
-            if t == 0:
-                factors[(grp, g)] = [
-                    stage.tile([P, PACK, GROUP * P], F32, name="factor_%d" % b) for b in range(2)
-                ]
-            turned = turned_banks[index]
-            column = g * PACK + t
-            for b in range(2):
-                gain = affine[:, (LN1_G, LN3_G)[b], column : column + 1]
-                shift = affine[:, (LN1_B, LN3_B)[b], column : column + 1]
-                if vector_helps and t == PACK - 1:
-                    nc.vector.tensor_scalar(
-                        out=factors[(grp, g)][b][:, t, :], in0=turned[:, b, :], scalar1=gain, scalar2=shift,
-                        op0=ALU.mult, op1=ALU.add,
-                    )
-                else:
-                    nc.scalar.activation(
-                        out=factors[(grp, g)][b][:, t, :], in_=turned[:, b, :], func=ACT.Identity,
-                        scale=gain, bias=shift,
-                    )
-
-        def multiply(half):
-            if not 0 <= half < GROUPS * PASSES:
-                return
-            grp, g = half // PASSES, half % PASSES
-            h_grouped = stage.tile([P, GROUP * P, PACK], BF16, align_bytes=64, name="h_grouped")
-            pieces = GROUP if half == GROUPS * PASSES - 1 else 1
-            width = GROUP * P // pieces
-            for piece in range(pieces):
-                tokens = slice(piece * width, (piece + 1) * width)
-                nc.vector.tensor_tensor(
-                    out=h_grouped[:, tokens, :].rearrange("p (c i) t -> p c t i", i=4),
-                    in0=factors[(grp, g)][0][:, :, tokens].rearrange("p t (c i) -> p c t i", i=4),
-                    in1=factors[(grp, g)][1][:, :, tokens].rearrange("p t (c i) -> p c t i", i=4),
-                    op=ALU.mult,
-                )
-            h_tiles[half] = h_grouped
-
-        def quantise_h(half):
-            if not 0 <= half < GROUPS * PASSES:
-                return
-            grp, g = half // PASSES, half % PASSES
-            pieces = GROUP if half == GROUPS * PASSES - 1 else 1
-            width = GROUP * P // pieces
-            for piece in range(pieces):
-                tokens = slice(piece * width, (piece + 1) * width)
-                nc.vector.quantize_mx(
-                    out=h_codes[:, grp, g, tokens].bitcast(FP8X4),
-                    scales=h_scales[:, grp, g, tokens],
-                    in_=h_tiles[half][:, tokens, :].rearrange("p w t -> p (w t)"),
+        def gain1(i, g):
+            gate1[(i, g)] = stage.tile([P, PACK, P], F32, name="gate1")
+            for t in range(PACK):
+                column = g * PACK + t
+                nc.scalar.activation(
+                    out=gate1[(i, g)][:, t, :], in_=turned_banks[(1, i, g)][:, t, :], func=ACT.Identity,
+                    scale=affine[:, LN1_G, column : column + 1], bias=affine[:, LN1_B, column : column + 1],
                 )
 
-        def project(i):
-            if not 0 <= i < TOKEN_TILES:
-                return
-            grp, j = i // GROUP, i % GROUP
-            tokens = slice(j * P, (j + 1) * P)
-            products[(2, i)] = mx_product(
-                h_codes[:, grp, :, tokens], h_scales[:, grp, :, tokens], c_words, c_planes, "y2"
+        def multiply(i, g):
+            h_tiles[(i, g)] = stage.tile([P, P, PACK], BF16, align_bytes=64, name="h_grouped")
+            nc.vector.tensor_tensor(
+                out=h_tiles[(i, g)][:].rearrange("p (c i) t -> p c t i", i=4),
+                in0=gate1[(i, g)][:].rearrange("p t (c i) -> p c t i", i=4),
+                in1=gate3[:, g * PACK : (g + 1) * PACK, i * P : (i + 1) * P].rearrange(
+                    "p t (c i) -> p c t i", i=4
+                ),
+                op=ALU.mult,
             )
 
+        def quantise_h(i, g):
+            nc.vector.quantize_mx(
+                out=h_codes[:, i, g, :].bitcast(FP8X4),
+                scales=h_scales[:, i, g, :],
+                in_=h_tiles[(i, g)][:].rearrange("p w t -> p (w t)"),
+            )
+
+        def project(i):
+            products[(2, i)] = mx_product(h_codes[:, i], h_scales[:, i], c_words, c_planes, "y2")
+
         def store(i):
-            if not 0 <= i < TOKEN_TILES:
-                return
             banks = products[(2, i)]
             result = stage.tile([P, BANKS, BANK], F32, name="result", bufs=4)
             for n in range(BANKS):
@@ -435,43 +458,50 @@ def tile_polymlp_skiplora_pa_kernel(
                 )
                 if i == TOKEN_TILES - 1:
                     nc.sync.dma_start(
-                        out=out_rows[i * P : (i + 1) * P, n * BANK : (n + 1) * BANK], in_=result[:, n, :]
+                        out=out_rows[:, i, n * BANK : (n + 1) * BANK], in_=result[:, n, :]
                     )
             if i < TOKEN_TILES - 1:
                 nc.sync.dma_start(
-                    out=out_rows[i * P : (i + 1) * P, :], in_=result[:].rearrange("q n c -> q (n c)")
+                    out=out_rows[:, i, :], in_=result[:].rearrange("q n c -> q (n c)")
                 )
 
-        PACE = 4
-        lags = {
-            "gains": -36, "spread": -36, "turn_x": -2, "copy_x": -1, "quantise_x": 2,
-            "product": {3: -3, 1: 3}, "add_bias": {3: -2, 1: 4}, "mean": {3: 0, 1: 5},
-            "deviation": {3: -1, 1: 6}, "normalise": {3: 0, 1: 7},
-            "turn": 16, "scale": 18, "multiply": 22, "quantise_h": 26, "project": 32, "store": 36,
-        }
+
         plan = []
 
         def put(position, stage_function, *which):
             plan.append((position, len(plan), stage_function, which))
 
+        HEAD = -100
+        for stage_function in (turn_z2, gram3, turn_vectors, bias_sums3):
+            put(HEAD, stage_function)
+        put(HEAD, spread_row, C_B, c_b, "q (t p) -> q t p", ("scalar", "scalar"))
+        for stage_function in (gram_bias3, gains_and_shifts, turn_u3):
+            put(HEAD, stage_function)
+        for q in range(3):
+            put(-17 + 2 * q, forms3, FORM_TILES * q)
+        put(0, finish3)
+        for half in range(2):
+            put(4 + 4 * half, spread_rstd3, half)
+        put(-8, spread_row, U1_B, u1_b, "q (p t) -> q t p", ("vector", "scalar"))
         for i in range(TOKEN_TILES):
-            for name, stage_function in (("turn_x", turn_x), ("copy_x", copy_x), ("quantise_x", quantise_x)):
-                put(lags[name] + PACE * i // 2, stage_function, i)
-            for branch in (3, 1):
-                for name, stage_function in (
-                    ("product", product), ("add_bias", add_bias), ("mean", mean), ("deviation", deviation), ("normalise", normalise)
+            for lag, stage_function in ((-20, turn_x), (-20, group_x), (-14, quantise_x)):
+                put(lag + 3 * i, stage_function, i)
+            for lag, stage_function in (
+                (-4, product1), (-3, add_bias1), (-2, mean1),
+                (1, deviation1), (13, normalise1),
+            ):
+                put(lag + 4 * i, stage_function, i)
+            if i % 4 == 0:
+                half = i // 4
+                for c in range(PASSES * PACK):
+                    for lag, stage_function in ((7, product3), (8, normalise3), (9, gain3)):
+                        put(lag + 14 * half + 1.5 * c, stage_function, c, half)
+            for g in range(PASSES):
+                for lag, stage_function in (
+                    (16, turn1), (17, gain1), (20, multiply), (24, quantise_h)
                 ):
-                    put(lags[name][branch] + PACE * i, stage_function, branch, i)
-        for k in range(GATE_BANKS):
-            put(lags["turn"] + k, turn, k)
-            put(lags["scale"] + k, scale, k, k < 22)
-        for half in range(GROUPS * PASSES):
-            put(lags["multiply"] + PACE * half, multiply, half)
-            put(lags["quantise_h"] + PACE * half, quantise_h, half)
-        for i in range(TOKEN_TILES):
-            put(lags["project"] + PACE * i, project, i)
-            put(lags["store"] + PACE * i, store, i)
-        put(lags["spread"], spread_row, C_B, c_b, "q (t p) -> q t p")
-        put(lags["gains"], gains_and_shifts)
+                    put(lag + 4 * i + 2 * g, stage_function, i, g)
+            put(30 + 4 * i, project, i)
+            put(30 + 4 * i, store, i)
         for position, order, stage_function, which in sorted(plan):
             stage_function(*which)

@@ -142,7 +142,6 @@ def tile_polymlp_skiplora_pa_kernel(
         c_b = keep.tile([P, BANKS, PACK, P], F32)
 
         z2T = keep.tile([P, TOKENS], BF16)
-        z2T_f32 = keep.tile([P, TOKENS], F32)
         u3T = keep.tile([P, PASSES * PACK, P], BF16)
 
         def turn_z2():
@@ -150,7 +149,6 @@ def tile_polymlp_skiplora_pa_kernel(
             for i in range(TOKEN_TILES):
                 nc.tensor.transpose(turned[:, i * P : (i + 1) * P], z2_sb[:, i, :], ident_bf16[:])
             nc.vector.tensor_copy(out=z2T[:], in_=turned[:])
-            nc.scalar.copy(out=z2T_f32[:], in_=turned[:])
 
         def turn_u3():
             turned = tp.tile([P, PASSES * PACK, P], BF16, name="u3T_ps", tag="tp")
@@ -187,7 +185,8 @@ def tile_polymlp_skiplora_pa_kernel(
         b_sums = keep.tile([P, 2], F32)
         ones_f32 = keep.tile([P, P], F32)
         nc.gpsimd.memset(ones_f32[:], 1.0)
-        form = keep.tile([P, DQ + 2], F32)
+        form_high = keep.tile([P, DQ + 2], BF16)
+        form_low = keep.tile([P, DQ + 2], BF16)
         b_means = keep.tile([P, 2], F32)
         square_eps = keep.tile([P, 1], F32)
         quadratic = keep.tile([P, TOKEN_TILES], F32)
@@ -225,7 +224,11 @@ def tile_polymlp_skiplora_pa_kernel(
                 )
             nc.tensor.matmul(out=gram[:, 256:258], lhsT=ones_f32[:], rhs=b_sums[:], start=True, stop=True)
             nc.scalar.activation(
-                out=form[:], in_=gram[:, 0 : DQ + 2], func=ACT.Identity, scale=1.0 / DH
+                out=form_high[:], in_=gram[:, 0 : DQ + 2], func=ACT.Identity, scale=1.0 / DH
+            )
+            nc.vector.scalar_tensor_tensor(
+                out=form_low[:], in0=gram[:, 0 : DQ + 2], scalar=1.0 / DH, in1=form_high[:], op0=ALU.mult,
+                op1=ALU.subtract,
             )
             nc.scalar.activation(
                 out=b_means[:], in_=gram[:, 256:258], func=ACT.Identity, scale=1.0 / DH
@@ -237,9 +240,11 @@ def tile_polymlp_skiplora_pa_kernel(
             tiles = range(first, min(first + FORM_TILES, TOKEN_TILES))
             bank = tp.tile([P, FORM_TILES, DQ + 2], F32, name="forms_ps", tag="tp")
             for j, i in enumerate(tiles):
-                nc.tensor.matmul(
-                    out=bank[:, j, :], lhsT=z2T_f32[:, i * P : (i + 1) * P], rhs=form[:], start=True, stop=True
-                )
+                for part in (form_high, form_low):
+                    nc.tensor.matmul(
+                        out=bank[:, j, :], lhsT=z2T[:, i * P : (i + 1) * P], rhs=part[:],
+                        start=(part is form_high), stop=(part is form_low),
+                    )
             for j, i in enumerate(tiles):
                 z_products = stage.tile([P, DQ], F32, name="z_products")
                 nc.vector.scalar_tensor_tensor(
@@ -370,7 +375,7 @@ def tile_polymlp_skiplora_pa_kernel(
 
         def add_bias1(i):
             rows[(1, i)] = keep.tile([P, PASSES, PACK, P], F32, name="rows1_%d" % i)
-            sums = stage.tile([P, PASSES], F32, name="sums", bufs=4)
+            sums = stage.tile([P, PASSES], F32, name="sums", bufs=8)
             for g in range(PASSES):
                 nc.vector.scalar_tensor_tensor(
                     out=rows[(1, i)][:, g], in0=products[(1, i)][g][:].rearrange("q (p t) -> q t p", t=PACK),
@@ -380,7 +385,7 @@ def tile_polymlp_skiplora_pa_kernel(
 
         def mean1(i):
             sums = stats[(1, i)]
-            neg_mean = stage.tile([P, 1], F32, name="neg_mean", bufs=4)
+            neg_mean = stage.tile([P, 1], F32, name="neg_mean", bufs=8)
             nc.vector.tensor_scalar(
                 out=neg_mean[:], in0=sums[:, 0:1], scalar1=sums[:, 1:2], scalar2=-1.0 / DH,
                 op0=ALU.add, op1=ALU.mult,
@@ -389,8 +394,8 @@ def tile_polymlp_skiplora_pa_kernel(
 
         def deviation1(i):
             neg_mean = stats[(1, i)]
-            sum_sq = stage.tile([P, 1], F32, name="sum_sq", bufs=4)
-            rstd = stage.tile([P, 1], F32, name="rstd1", bufs=4)
+            sum_sq = stage.tile([P, 1], F32, name="sum_sq", bufs=8)
+            rstd = stage.tile([P, 1], F32, name="rstd1", bufs=8)
             squares = stage.tile([P, DH], BF16, name="squares")
             nc.scalar.activation(
                 out=squares[:], in_=rows[(1, i)][:].rearrange("q g t p -> q (g t p)"),
@@ -487,7 +492,7 @@ def tile_polymlp_skiplora_pa_kernel(
             for lag, stage_function in ((-20, turn_x), (-20, group_x), (-14, quantise_x)):
                 put(lag + 3 * i, stage_function, i)
             for lag, stage_function in (
-                (-4, product1), (-3, add_bias1), (-2, mean1),
+                (-4, product1), (-3, add_bias1), (-1, mean1),
                 (1, deviation1), (13, normalise1),
             ):
                 put(lag + 4 * i, stage_function, i)

@@ -285,8 +285,8 @@ def tile_polymlp_skiplora_pa_kernel(
 
         x_codes = keep.tile([P, TOKEN_TILES, PASSES, P], U32, align_bytes=64)
         x_scales = keep.tile([P, TOKEN_TILES, PASSES, P], U8, align_bytes=64)
-        h_codes = keep.tile([P, TOKEN_TILES, PASSES, P], U32, align_bytes=64)
-        h_scales = keep.tile([P, TOKEN_TILES, PASSES, P], U8, align_bytes=64)
+        h_codes = keep.tile([P, PASSES, TOKENS], U32, align_bytes=64)
+        h_scales = keep.tile([P, PASSES, TOKENS], U8, align_bytes=64)
 
         x_turned = {}
         x_tiles = {}
@@ -414,44 +414,56 @@ def tile_polymlp_skiplora_pa_kernel(
                 op0=ALU.add, op1=ALU.mult,
             )
 
+        gate_tiles = [(0, 1), (2, 3), (4, 5), (6,), (7,)]
         gate1 = {}
         h_tiles = {}
 
-        def turn1(i, g):
-            turned = tp.tile([P, PACK, P], F32, name="turned1", tag="tp")
-            for t in range(PACK):
-                nc.tensor.transpose(turned[:, t, :], rows[(1, i)][:, g, t, :], ident_f32[:])
-            turned_banks[(1, i, g)] = turned
+        def tokens_of(u):
+            return slice(gate_tiles[u][0] * P, (gate_tiles[u][-1] + 1) * P)
 
-        def gain1(i, g):
-            gate1[(i, g)] = stage.tile([P, PACK, P], F32, name="gate1")
+        def turn1(u, g):
+            tiles = gate_tiles[u]
+            columns = PACK // len(tiles)
+            for b in range(len(tiles)):
+                turned = tp.tile([P, columns, len(tiles) * P], F32, name="turned1", tag="tp")
+                for s in range(columns):
+                    for j, i in enumerate(tiles):
+                        nc.tensor.transpose(
+                            turned[:, s, j * P : (j + 1) * P], rows[(1, i)][:, g, columns * b + s, :], ident_f32[:]
+                        )
+                turned_banks[(1, u, g, b)] = turned
+
+        def gain1(u, g):
+            tiles = gate_tiles[u]
+            columns = PACK // len(tiles)
+            gate1[(u, g)] = stage.tile([P, PACK, len(tiles) * P], F32, name="gate1")
             for t in range(PACK):
                 column = g * PACK + t
                 nc.scalar.activation(
-                    out=gate1[(i, g)][:, t, :], in_=turned_banks[(1, i, g)][:, t, :], func=ACT.Identity,
-                    scale=affine[:, LN1_G, column : column + 1], bias=affine[:, LN1_B, column : column + 1],
+                    out=gate1[(u, g)][:, t, :], in_=turned_banks[(1, u, g, t // columns)][:, t % columns, :],
+                    func=ACT.Identity, scale=affine[:, LN1_G, column : column + 1],
+                    bias=affine[:, LN1_B, column : column + 1],
                 )
 
-        def multiply(i, g):
-            h_tiles[(i, g)] = stage.tile([P, P, PACK], BF16, align_bytes=64, name="h_grouped")
+        def multiply(u, g):
+            h_tiles[(u, g)] = stage.tile([P, len(gate_tiles[u]) * P, PACK], BF16, align_bytes=64, name="h_grouped")
             nc.vector.tensor_tensor(
-                out=h_tiles[(i, g)][:].rearrange("p (c i) t -> p c t i", i=4),
-                in0=gate1[(i, g)][:].rearrange("p t (c i) -> p c t i", i=4),
-                in1=gate3[:, g * PACK : (g + 1) * PACK, i * P : (i + 1) * P].rearrange(
-                    "p t (c i) -> p c t i", i=4
-                ),
+                out=h_tiles[(u, g)][:].rearrange("p (c i) t -> p c t i", i=4),
+                in0=gate1[(u, g)][:].rearrange("p t (c i) -> p c t i", i=4),
+                in1=gate3[:, g * PACK : (g + 1) * PACK, tokens_of(u)].rearrange("p t (c i) -> p c t i", i=4),
                 op=ALU.mult,
             )
 
-        def quantise_h(i, g):
+        def quantise_h(u, g):
             nc.vector.quantize_mx(
-                out=h_codes[:, i, g, :].bitcast(FP8X4),
-                scales=h_scales[:, i, g, :],
-                in_=h_tiles[(i, g)][:].rearrange("p w t -> p (w t)"),
+                out=h_codes[:, g, tokens_of(u)].bitcast(FP8X4),
+                scales=h_scales[:, g, tokens_of(u)],
+                in_=h_tiles[(u, g)][:].rearrange("p w t -> p (w t)"),
             )
 
         def project(i):
-            products[(2, i)] = mx_product(h_codes[:, i], h_scales[:, i], c_words, c_planes, "y2")
+            tokens = slice(i * P, (i + 1) * P)
+            products[(2, i)] = mx_product(h_codes[:, :, tokens], h_scales[:, :, tokens], c_words, c_planes, "y2")
 
         def store(i):
             banks = products[(2, i)]
@@ -477,36 +489,39 @@ def tile_polymlp_skiplora_pa_kernel(
             plan.append((position, len(plan), stage_function, which))
 
         HEAD = -100
-        for stage_function in (turn_z2, gram3, turn_vectors, bias_sums3):
+        for stage_function in (turn_z2, gram3, turn_vectors):
             put(HEAD, stage_function)
         put(HEAD, spread_row, C_B, c_b, "q (t p) -> q t p", ("scalar", "scalar"))
-        for stage_function in (gram_bias3, gains_and_shifts, turn_u3):
+        for stage_function in (bias_sums3, gram_bias3, turn_u3):
             put(HEAD, stage_function)
+        put(3, gains_and_shifts)
         for q in range(3):
-            put(-17 + 2 * q, forms3, FORM_TILES * q)
-        put(0, finish3)
+            put(-35 + 2 * q, forms3, FORM_TILES * q)
+        put(9, finish3)
         for half in range(2):
-            put(4 + 4 * half, spread_rstd3, half)
-        put(-8, spread_row, U1_B, u1_b, "q (p t) -> q t p", ("vector", "scalar"))
+            put(15 + 4 * half, spread_rstd3, half)
+        put(-2, spread_row, U1_B, u1_b, "q (p t) -> q t p", ("vector", "scalar"))
         for i in range(TOKEN_TILES):
-            for lag, stage_function in ((-20, turn_x), (-20, group_x), (-14, quantise_x)):
+            for lag, stage_function in ((-8, turn_x), (-6, group_x), (-2, quantise_x)):
                 put(lag + 3 * i, stage_function, i)
             for lag, stage_function in (
-                (-4, product1), (-3, add_bias1), (-1, mean1),
-                (1, deviation1), (13, normalise1),
+                (7, product1), (9, add_bias1), (12, mean1),
+                (14, deviation1), (17, normalise1),
             ):
                 put(lag + 4 * i, stage_function, i)
             if i % 4 == 0:
                 half = i // 4
                 for c in range(PASSES * PACK):
-                    for lag, stage_function in ((7, product3), (8, normalise3), (9, gain3)):
+                    for lag, stage_function in ((22, product3), (24, normalise3), (25, gain3)):
                         put(lag + 14 * half + 1.5 * c, stage_function, c, half)
+        for u, tiles in enumerate(gate_tiles):
             for g in range(PASSES):
                 for lag, stage_function in (
-                    (16, turn1), (17, gain1), (20, multiply), (24, quantise_h)
+                    (27, turn1), (28, gain1), (32, multiply), (35, quantise_h)
                 ):
-                    put(lag + 4 * i + 2 * g, stage_function, i, g)
-            put(30 + 4 * i, project, i)
-            put(30 + 4 * i, store, i)
+                    put(lag + 4 * tiles[-1] + 2 * len(tiles) * g, stage_function, u, g)
+            for i in tiles:
+                put(45 + 4 * i, project, i)
+                put(47 + 4 * i, store, i)
         for position, order, stage_function, which in sorted(plan):
             stage_function(*which)

@@ -64,6 +64,14 @@ def tile_polymlp_skiplora_pa_kernel(
         tp = stack.enter_context(tc.psum_pool(name="tp", bufs=4))
 
 
+        zeros = keep.tile([P, BANK], BF16)
+        nc.gpsimd.memset(zeros[:].bitcast(I32), 0)
+
+        def warm_up():
+            for q in range(3):
+                bank = acc.tile([P, BANK], F32, name="warm_bank", tag="acc")
+                nc.tensor.matmul(out=bank[:], lhsT=zeros[:, 0:P], rhs=zeros[:], start=True, stop=True)
+
         vectors = (U3_b, ln1_g, ln1_b, ln3_g, ln3_b, U1_b, C_b)
         U3_B, LN1_G, LN1_B, LN3_G, LN3_B, U1_B, C_B = range(len(vectors))
         vector_rows = keep.tile([P, DH], BF16)
@@ -461,6 +469,15 @@ def tile_polymlp_skiplora_pa_kernel(
                 in_=h_tiles[(u, g)][:].rearrange("p w t -> p (w t)"),
             )
 
+        def fill(i):
+            bank = tp.tile([P, BANK], F32, name="fill_bank", tag="tp")
+            for q in range(2):
+                nc.tensor.matmul_mx(
+                    out=bank[:], lhsT=x_codes[:, i, 0, :].bitcast(FP8X4), lhsT_scale=x_scales[:, i, 0, :],
+                    rhs=c_words[:, 0, 0 : PACK * BANK].bitcast(FP8X4), rhs_scale=c_planes[0:P, 0:BANK],
+                    start=True, stop=True,
+                )
+
         def project(i):
             tokens = slice(i * P, (i + 1) * P)
             products[(2, i)] = mx_product(h_codes[:, :, tokens], h_scales[:, :, tokens], c_words, c_planes, "y2")
@@ -488,25 +505,27 @@ def tile_polymlp_skiplora_pa_kernel(
         def put(position, stage_function, *which):
             plan.append((position, len(plan), stage_function, which))
 
-        HEAD = -100
-        for stage_function in (turn_z2, gram3, turn_vectors):
-            put(HEAD, stage_function)
-        put(HEAD, spread_row, C_B, c_b, "q (t p) -> q t p", ("scalar", "scalar"))
-        for stage_function in (bias_sums3, gram_bias3, turn_u3):
-            put(HEAD, stage_function)
-        put(3, gains_and_shifts)
+        put(-405, warm_up)
+        put(-216, turn_z2)
+        put(-154, turn_vectors)
+        put(-8, turn_u3)
+        put(-10, gains_and_shifts)
+        put(-150, bias_sums3)
+        put(-167, gram3)
+        put(-25, gram_bias3)
         for q in range(3):
-            put(-35 + 2 * q, forms3, FORM_TILES * q)
-        put(9, finish3)
+            put(-8 + 2 * q, forms3, FORM_TILES * q)
+        put(2, finish3)
         for half in range(2):
-            put(15 + 4 * half, spread_rstd3, half)
-        put(-2, spread_row, U1_B, u1_b, "q (p t) -> q t p", ("vector", "scalar"))
+            put(19 + 4 * half, spread_rstd3, half)
+        put(-5, spread_row, U1_B, u1_b, "q (p t) -> q t p", ("vector", "scalar"))
+        put(-139, spread_row, C_B, c_b, "q (t p) -> q t p", ("scalar", "scalar"))
         for i in range(TOKEN_TILES):
-            for lag, stage_function in ((-8, turn_x), (-6, group_x), (-2, quantise_x)):
+            for lag, stage_function in ((-9, turn_x), (-9, group_x), (-1, quantise_x)):
                 put(lag + 3 * i, stage_function, i)
             for lag, stage_function in (
-                (7, product1), (9, add_bias1), (12, mean1),
-                (14, deviation1), (17, normalise1),
+                (9, product1), (11, add_bias1), (14, mean1),
+                (14, deviation1), (27, normalise1),
             ):
                 put(lag + 4 * i, stage_function, i)
             if i % 4 == 0:
@@ -514,14 +533,17 @@ def tile_polymlp_skiplora_pa_kernel(
                 for c in range(PASSES * PACK):
                     for lag, stage_function in ((22, product3), (24, normalise3), (25, gain3)):
                         put(lag + 14 * half + 1.5 * c, stage_function, c, half)
-        for u, tiles in enumerate(gate_tiles):
-            for g in range(PASSES):
-                for lag, stage_function in (
-                    (27, turn1), (28, gain1), (32, multiply), (35, quantise_h)
-                ):
-                    put(lag + 4 * tiles[-1] + 2 * len(tiles) * g, stage_function, u, g)
-            for i in tiles:
-                put(45 + 4 * i, project, i)
-                put(47 + 4 * i, store, i)
+            for u, tiles in enumerate(gate_tiles):
+                if tiles[-1] == i:
+                    for g in range(PASSES):
+                        for lag, stage_function in (
+                            (27, turn1), (28, gain1), (32, multiply), (36, quantise_h)
+                        ):
+                            put(lag + 4 * i + 2 * len(tiles) * g, stage_function, u, g)
+                    for j in tiles:
+                        if j in (4, 6):
+                            put(30 + 4 * j, fill, j)
+                        put(44 + 4 * j, project, j)
+                        put(47 + 4 * j, store, j)
         for position, order, stage_function, which in sorted(plan):
             stage_function(*which)

@@ -64,14 +64,6 @@ def tile_polymlp_skiplora_pa_kernel(
         tp = stack.enter_context(tc.psum_pool(name="tp", bufs=4))
 
 
-        zeros = keep.tile([P, BANK], BF16)
-        nc.gpsimd.memset(zeros[:].bitcast(I32), 0)
-
-        def warm_up():
-            for q in range(3):
-                bank = acc.tile([P, BANK], F32, name="warm_bank", tag="acc")
-                nc.tensor.matmul(out=bank[:], lhsT=zeros[:, 0:P], rhs=zeros[:], start=True, stop=True)
-
         vectors = (U3_b, ln1_g, ln1_b, ln3_g, ln3_b, U1_b, C_b)
         U3_B, LN1_G, LN1_B, LN3_G, LN3_B, U1_B, C_B = range(len(vectors))
         vector_rows = keep.tile([P, DH], BF16)
@@ -469,15 +461,6 @@ def tile_polymlp_skiplora_pa_kernel(
                 in_=h_tiles[(u, g)][:].rearrange("p w t -> p (w t)"),
             )
 
-        def fill(i):
-            bank = tp.tile([P, BANK], F32, name="fill_bank", tag="tp")
-            for q in range(2):
-                nc.tensor.matmul_mx(
-                    out=bank[:], lhsT=x_codes[:, i, 0, :].bitcast(FP8X4), lhsT_scale=x_scales[:, i, 0, :],
-                    rhs=c_words[:, 0, 0 : PACK * BANK].bitcast(FP8X4), rhs_scale=c_planes[0:P, 0:BANK],
-                    start=True, stop=True,
-                )
-
         def project(i):
             tokens = slice(i * P, (i + 1) * P)
             products[(2, i)] = mx_product(h_codes[:, :, tokens], h_scales[:, :, tokens], c_words, c_planes, "y2")
@@ -505,7 +488,6 @@ def tile_polymlp_skiplora_pa_kernel(
         def put(position, stage_function, *which):
             plan.append((position, len(plan), stage_function, which))
 
-        put(-405, warm_up)
         put(-216, turn_z2)
         put(-154, turn_vectors)
         put(-8, turn_u3)
@@ -541,8 +523,6 @@ def tile_polymlp_skiplora_pa_kernel(
                         ):
                             put(lag + 4 * i + 2 * len(tiles) * g, stage_function, u, g)
                     for j in tiles:
-                        if j in (4, 6):
-                            put(30 + 4 * j, fill, j)
                         put(44 + 4 * j, project, j)
                         put(47 + 4 * j, store, j)
         for position, order, stage_function, which in sorted(plan):

from contextlib import ExitStack

import concourse.mybir as mybir
from concourse.masks import make_identity

F32 = mybir.dt.float32
BF16 = mybir.dt.bfloat16
I32 = mybir.dt.int32
U32 = mybir.dt.uint32
U8 = mybir.dt.uint8
FP8X4 = mybir.dt.float8_e4m3fn_x4
ALU = mybir.AluOpType
ACT = mybir.ActivationFunctionType

P = 128
PACK = 4
K_PASS = P * PACK
BANK = 512
QUADRANTS = 4

TOKENS = 1024
D = 1024
DH = 1024
DQ = 128
EPS = 1e-6

TOKEN_TILES = TOKENS // P
PASSES = DH // K_PASS
BANKS = DH // BANK
PAIR = 2

FLOPS = 2 * TOKENS * (D * DH + DQ * DH + DH * D)


def tile_polymlp_skiplora_pa_kernel(
    tc,
    x,
    z2,
    U1_w_words,
    U1_w_scales,
    U1_b,
    U3_w,
    U3_b,
    C_w_words,
    C_w_scales,
    C_b,
    ln1_g,
    ln1_b,
    ln3_g,
    ln3_b,
    alpha,
    out,
):
    nc = tc.nc
    x_rows = x.flatten_outer_dims().rearrange("(p i) d -> p i d", i=TOKEN_TILES)
    z2_rows = z2.flatten_outer_dims().rearrange("(p i) d -> p i d", i=TOKEN_TILES)
    out_rows = out.flatten_outer_dims().rearrange("(p i) d -> p i d", i=TOKEN_TILES)

    with ExitStack() as stack:
        keep = stack.enter_context(tc.tile_pool(name="keep", bufs=1))
        stage = stack.enter_context(tc.tile_pool(name="stage", bufs=3))
        stack.enter_context(tc.manual_schedule())
        acc = stack.enter_context(tc.psum_pool(name="acc", bufs=4))
        tp = stack.enter_context(tc.psum_pool(name="tp", bufs=4))


        vectors = (U3_b, ln1_g, ln1_b, ln3_g, ln3_b, U1_b, C_b)
        U3_B, LN1_G, LN1_B, LN3_G, LN3_B, U1_B, C_B = range(len(vectors))
        vector_rows = keep.tile([P, DH], BF16)
        nc.vector.memset(vector_rows[:].bitcast(I32), 0)

        u1_planes = keep.tile([P, DH], U8, align_bytes=64)
        nc.vector.memset(u1_planes[:].bitcast(I32), 0)
        c_planes = keep.tile([P, D], U8, align_bytes=64)
        nc.gpsimd.memset(c_planes[:].bitcast(I32), 0)

        def load_scales(scales_dram, planes):
            for quadrant in range(QUADRANTS):
                first_row = 32 * quadrant
                nc.sync.dma_start(
                    out=planes[first_row : first_row + 4 * PASSES, :].bitcast(I32),
                    in_=scales_dram[:, 4 * quadrant : 4 * quadrant + 4, :].bitcast(I32),
                )

        def load_words(words_dram, name):
            words_sb = keep.tile([P, PASSES, PACK * DH], U8, align_bytes=64, name=name)
            for g in range(PASSES):
                nc.sync.dma_start(
                    out=words_sb[:, g, :].bitcast(I32),
                    in_=words_dram[g].rearrange("p n t -> p (n t)").bitcast(I32),
                )
            return words_sb

        x_sb = keep.tile([P, TOKEN_TILES, D], BF16)

        def load_x(i):
            nc.sync.dma_start(out=x_sb[:, i, :], in_=x_rows[:, i, :])

        z2_sb = keep.tile([P, TOKEN_TILES, DQ], BF16)
        nc.scalar.dma_start(out=z2_sb[:], in_=z2_rows)
        u3_sb = keep.tile([P, PASSES * PACK, DQ], BF16)
        nc.scalar.dma_start(
            out=u3_sb[:].rearrange("p (g t) d -> p g t d", g=PASSES),
            in_=U3_w.rearrange("(g p t) d -> p g t d", g=PASSES, t=PACK),
        )
        eps = keep.tile([P, 1], F32)
        nc.vector.memset(eps[:], EPS)
        first_rstd = keep.tile([P, 1], F32)
        nc.scalar.activation(
            out=first_rstd[:], in_=eps[:], func=ACT.Abs_reciprocal_sqrt, bias=eps[:, 0:1], scale=1.0
        )
        for r, vector in enumerate(vectors):
            nc.sync.dma_start(out=vector_rows[r : r + 1, :], in_=vector.rearrange("(o n) -> o n", o=1))
        alpha_raw = keep.tile([P, 1], BF16)
        nc.sync.dma_start(out=alpha_raw[:], in_=alpha.partition_broadcast(P))
        load_scales(U1_w_scales, u1_planes)
        load_x(0)
        w1_words = load_words(U1_w_words, "w1_words")
        for i in range(1, TOKEN_TILES):
            load_x(i)
        load_scales(C_w_scales, c_planes)
        c_words = load_words(C_w_words, "c_words")

        ident_bf16 = keep.tile([P, P], BF16)
        make_identity(nc, ident_bf16[:])
        ident_f32 = keep.tile([P, P], F32)
        nc.vector.tensor_copy(out=ident_f32[:], in_=ident_bf16[:])

        def spread_row(r, spread, pattern, engines):
            for n in range(BANKS):
                bank = acc.tile([P, BANK], F32, name="row_bank", tag="acc")
                nc.tensor.matmul(
                    out=bank[:], lhsT=ident_bf16[:, r : r + 1].to_broadcast([P, P]),
                    rhs=vector_rows[:, BANK * n : BANK * (n + 1)], start=True, stop=True,
                )
                if engines[n] == "vector":
                    nc.vector.tensor_copy(out=spread[:, n], in_=bank[:].rearrange(pattern, t=PACK))
                else:
                    nc.scalar.copy(out=spread[:, n], in_=bank[:].rearrange(pattern, t=PACK))

        u1_b = keep.tile([P, PASSES, PACK, P], F32)
        c_b = keep.tile([P, BANKS, PACK, P], F32)

        z2T = keep.tile([P, TOKENS], BF16)
        u3T = keep.tile([P, PASSES * PACK, P], BF16)

        def turn_z2():
            turned = tp.tile([P, TOKENS], BF16, name="z2T_ps", tag="tp")
            for i in range(TOKEN_TILES):
                nc.tensor.transpose(turned[:, i * P : (i + 1) * P], z2_sb[:, i, :], ident_bf16[:])
            nc.vector.tensor_copy(out=z2T[:], in_=turned[:])

        def turn_u3():
            turned = tp.tile([P, PASSES * PACK, P], BF16, name="u3T_ps", tag="tp")
            for c in range(PASSES * PACK):
                nc.tensor.transpose(turned[:, c, :], u3_sb[:, c, :], ident_bf16[:])
            nc.scalar.copy(out=u3T[:], in_=turned[:])

        affine = keep.tile([P, 5, PASSES * PACK], F32)

        def turn_vectors():
            turned = tp.tile([P, PASSES * PACK, P], BF16, name="vectors_ps", tag="tp")
            for g in range(PASSES):
                for t in range(PACK):
                    nc.tensor.transpose(
                        turned[:, g * PACK + t, :], vector_rows[:, K_PASS * g + t : K_PASS * (g + 1) : PACK],
                        ident_bf16[:],
                    )
            nc.vector.tensor_copy(out=affine[:], in_=turned[:, :, 0:5].rearrange("p c r -> p r c"))

        def gains_and_shifts():
            alpha_f32 = keep.tile([P, 1], F32)
            nc.vector.tensor_copy(out=alpha_f32[:], in_=alpha_raw[:])
            nc.vector.tensor_scalar(
                out=affine[:, LN3_G, :], in0=affine[:, LN3_G, :], scalar1=alpha_f32[:, 0:1], scalar2=None,
                op0=ALU.mult,
            )
            nc.vector.tensor_scalar(
                out=affine[:, LN3_B, :], in0=affine[:, LN3_B, :], scalar1=alpha_f32[:, 0:1], scalar2=1.0,
                op0=ALU.mult, op1=ALU.add,
            )

        b_and_one = keep.tile([P, PASSES * PACK, 2], BF16)
        nc.gpsimd.memset(b_and_one[:], 1.0)
        b_sums = keep.tile([P, 2], F32)
        ones_f32 = keep.tile([P, P], F32)
        nc.gpsimd.memset(ones_f32[:], 1.0)
        form_high = keep.tile([P, DQ + 2], BF16)
        form_low = keep.tile([P, DQ + 2], BF16)
        b_means = keep.tile([P, 2], F32)
        square_eps = keep.tile([P, 1], F32)
        quadratic = keep.tile([P, TOKEN_TILES], F32)
        linear = keep.tile([P, TOKEN_TILES, 2], F32)
        neg_mean3 = keep.tile([P, TOKEN_TILES], F32)
        rstd3 = keep.tile([P, TOKEN_TILES], F32)
        rstd3_row = keep.tile([P, TOKENS], F32)
        gram_banks = {}

        def bias_sums3():
            column = affine[:, U3_B, :]
            nc.vector.tensor_copy(out=b_and_one[:, :, 0], in_=column)
            squares = stage.tile([P, PASSES * PACK], F32, name="b_squares")
            nc.vector.reduce_sum(out=b_sums[:, 0:1], in_=column, axis=mybir.AxisListType.X)
            nc.vector.scalar_tensor_tensor(
                out=squares[:], in0=column, scalar=1.0, in1=column, op0=ALU.mult, op1=ALU.mult,
                accum_out=b_sums[:, 1:2],
            )

        def gram3():
            gram = tp.tile([P, BANK], F32, name="gram_ps", tag="tp")
            for c in range(PASSES * PACK):
                nc.tensor.matmul(
                    out=gram[:, 0:DQ], lhsT=u3_sb[:, c, :], rhs=u3_sb[:, c, :],
                    start=(c == 0), stop=(c == PASSES * PACK - 1),
                )
            gram_banks[0] = gram

        def gram_bias3():
            gram = gram_banks[0]
            for c in range(PASSES * PACK):
                nc.tensor.matmul(
                    out=gram[:, DQ : DQ + 2], lhsT=u3_sb[:, c, :], rhs=b_and_one[:, c, :],
                    start=(c == 0), stop=(c == PASSES * PACK - 1),
                )
            nc.tensor.matmul(out=gram[:, 256:258], lhsT=ones_f32[:], rhs=b_sums[:], start=True, stop=True)
            nc.scalar.activation(
                out=form_high[:], in_=gram[:, 0 : DQ + 2], func=ACT.Identity, scale=1.0 / DH
            )
            nc.vector.scalar_tensor_tensor(
                out=form_low[:], in0=gram[:, 0 : DQ + 2], scalar=1.0 / DH, in1=form_high[:], op0=ALU.mult,
                op1=ALU.subtract,
            )
            nc.scalar.activation(
                out=b_means[:], in_=gram[:, 256:258], func=ACT.Identity, scale=1.0 / DH
            )

        FORM_TILES = 3

        def forms3(first):
            tiles = range(first, min(first + FORM_TILES, TOKEN_TILES))
            bank = tp.tile([P, FORM_TILES, DQ + 2], F32, name="forms_ps", tag="tp")
            for j, i in enumerate(tiles):
                for part in (form_high, form_low):
                    nc.tensor.matmul(
                        out=bank[:, j, :], lhsT=z2T[:, i * P : (i + 1) * P], rhs=part[:],
                        start=(part is form_high), stop=(part is form_low),
                    )
            for j, i in enumerate(tiles):
                z_products = stage.tile([P, DQ], F32, name="z_products")
                nc.vector.scalar_tensor_tensor(
                    out=z_products[:], in0=bank[:, j, 0:DQ], scalar=1.0, in1=z2_sb[:, i, :], op0=ALU.mult,
                    op1=ALU.mult, accum_out=quadratic[:, i : i + 1],
                )
            nc.scalar.copy(
                out=linear[:, first : first + len(tiles), :], in_=bank[:, 0 : len(tiles), DQ : DQ + 2]
            )

        def finish3():
            mean_square = keep.tile([P, TOKEN_TILES], F32)
            square_mean = keep.tile([P, TOKEN_TILES], F32)
            variance = keep.tile([P, TOKEN_TILES], F32)
            nc.vector.tensor_scalar(
                out=neg_mean3[:], in0=linear[:, :, 1], scalar1=b_means[:, 0:1], scalar2=-1.0, op0=ALU.add, op1=ALU.mult
            )
            nc.vector.scalar_tensor_tensor(
                out=mean_square[:], in0=linear[:, :, 0], scalar=2.0, in1=quadratic[:], op0=ALU.mult, op1=ALU.add
            )
            nc.vector.tensor_scalar(
                out=square_eps[:], in0=b_means[:, 1:2], scalar1=EPS, scalar2=None, op0=ALU.add
            )
            nc.vector.tensor_tensor(out=square_mean[:], in0=neg_mean3[:], in1=neg_mean3[:], op=ALU.mult)
            nc.vector.tensor_tensor(out=variance[:], in0=mean_square[:], in1=square_mean[:], op=ALU.subtract)
            nc.scalar.activation(
                out=rstd3[:], in_=variance[:], func=ACT.Abs_reciprocal_sqrt, bias=square_eps[:, 0:1], scale=1.0
            )

        def spread_rstd3(half):
            spread = tp.tile([P, BANK], F32, name="rstd_ps", tag="tp")
            for j in range(BANK // P):
                i = half * (BANK // P) + j
                nc.tensor.transpose(
                    spread[:, j * P : (j + 1) * P], rstd3[:, i : i + 1].to_broadcast([P, P]), ident_f32[:]
                )
            nc.scalar.copy(out=rstd3_row[:, half * BANK : (half + 1) * BANK], in_=spread[:])

        x_codes = keep.tile([P, TOKEN_TILES, PASSES, P], U32, align_bytes=64)
        x_scales = keep.tile([P, TOKEN_TILES, PASSES, P], U8, align_bytes=64)
        h_codes = keep.tile([P, PASSES, TOKENS], U32, align_bytes=64)
        h_scales = keep.tile([P, PASSES, TOKENS], U8, align_bytes=64)

        x_turned = {}
        x_tiles = {}

        def turn_x(i):
            words = x_sb[:, i, :].bitcast(F32)
            x_turned[i] = tp.tile([P, PASSES, 2, P], F32, name="xT", tag="tp")
            for g in range(PASSES):
                for u in range(2):
                    first = (K_PASS // 2) * g + u
                    nc.tensor.transpose(
                        x_turned[i][:, g, u, :], words[:, first : (K_PASS // 2) * (g + 1) : 2], ident_f32[:]
                    )

        def group_x(i):
            x_tiles[i] = stage.tile([P, PASSES, P, PACK], BF16, align_bytes=64, name="x_grouped")
            nc.scalar.copy(
                out=x_tiles[i][:].bitcast(F32), in_=x_turned[i][:].rearrange("p g u w -> p g w u")
            )

        def quantise_x(i):
            nc.vector.quantize_mx(
                out=x_codes[:, i].rearrange("p g w -> p (g w)").bitcast(FP8X4),
                scales=x_scales[:, i].rearrange("p g w -> p (g w)"),
                in_=x_tiles[i][:].rearrange("p g w t -> p (g w t)"),
            )

        def mx_product(codes, scales, weight_words, planes, name):
            banks = [acc.tile([P, BANK], F32, name="%s_%d" % (name, n), tag="acc") for n in range(BANKS)]
            for n in range(BANKS):
                for g in range(PASSES):
                    plane_row = 4 * g
                    nc.tensor.matmul_mx(
                        out=banks[n][:],
                        lhsT=codes[:, g, :].bitcast(FP8X4),
                        lhsT_scale=scales[:, g, :],
                        rhs=weight_words[:, g, PACK * BANK * n : PACK * BANK * (n + 1)].bitcast(FP8X4),
                        rhs_scale=planes[plane_row:P, BANK * n : BANK * (n + 1)],
                        start=(g == 0),
                        stop=(g == PASSES - 1),
                    )
            return banks

        def add_transposed(bank, first, column, last):
            nc.tensor.matmul(
                out=bank[:, first : first + P], lhsT=column.to_broadcast([P, P]), rhs=ident_f32[:],
                start=False, stop=last, is_transpose=True,
            )

        rows = {}
        products = {}
        stats = {}

        gate3 = keep.tile([P, PASSES * PACK, TOKENS], F32)
        turned_banks = {}

        def product3(c, half):
            bank = tp.tile([P, BANK], F32, name="y3", tag="tp")
            nc.tensor.matmul(
                out=bank[:], lhsT=u3T[:, c, :], rhs=z2T[:, half * BANK : (half + 1) * BANK], start=True, stop=False
            )
            tiles = BANK // P
            for j in range(tiles):
                i = half * tiles + j
                add_transposed(bank, j * P, neg_mean3[:, i : i + 1], j == tiles - 1)
            turned_banks[(3, c, half)] = bank

        normal3 = {}

        def normalise3(c, half):
            normal3[(c, half)] = stage.tile([P, BANK], F32, name="normal3")
            row = rstd3_row[:, half * BANK : (half + 1) * BANK]
            nc.vector.scalar_tensor_tensor(
                out=normal3[(c, half)][:], in0=turned_banks[(3, c, half)][:], scalar=affine[:, U3_B, c : c + 1],
                in1=row, op0=ALU.add, op1=ALU.mult,
            )

        def gain3(c, half):
            nc.scalar.activation(
                out=gate3[:, c, half * BANK : (half + 1) * BANK], in_=normal3[(c, half)][:], func=ACT.Identity,
                scale=affine[:, LN3_G, c : c + 1], bias=affine[:, LN3_B, c : c + 1],
            )

        def product1(i):
            products[(1, i)] = mx_product(x_codes[:, i], x_scales[:, i], w1_words, u1_planes, "y1")

        def add_bias1(i):
            rows[(1, i)] = keep.tile([P, PASSES, PACK, P], F32, name="rows1_%d" % i)
            sums = stage.tile([P, PASSES], F32, name="sums", bufs=8)
            for g in range(PASSES):
                nc.vector.scalar_tensor_tensor(
                    out=rows[(1, i)][:, g], in0=products[(1, i)][g][:].rearrange("q (p t) -> q t p", t=PACK),
                    scalar=1.0, in1=u1_b[:, g], op0=ALU.mult, op1=ALU.add, accum_out=sums[:, g : g + 1],
                )
            stats[(1, i)] = sums

        def mean1(i):
            sums = stats[(1, i)]
            neg_mean = stage.tile([P, 1], F32, name="neg_mean", bufs=8)
            nc.vector.tensor_scalar(
                out=neg_mean[:], in0=sums[:, 0:1], scalar1=sums[:, 1:2], scalar2=-1.0 / DH,
                op0=ALU.add, op1=ALU.mult,
            )
            stats[(1, i)] = neg_mean

        def deviation1(i):
            neg_mean = stats[(1, i)]
            sum_sq = stage.tile([P, 1], F32, name="sum_sq", bufs=8)
            rstd = stage.tile([P, 1], F32, name="rstd1", bufs=8)
            squares = stage.tile([P, DH], BF16, name="squares")
            nc.scalar.activation(
                out=squares[:], in_=rows[(1, i)][:].rearrange("q g t p -> q (g t p)"),
                func=ACT.Square, bias=neg_mean[:, 0:1], scale=1.0, accum_out=sum_sq[:, 0:1],
            )
            nc.scalar.activation(
                out=rstd[:], in_=sum_sq[:], func=ACT.Abs_reciprocal_sqrt, bias=eps[:, 0:1], scale=1.0 / DH
            )
            stats[(1, i)] = (neg_mean, rstd)

        def normalise1(i):
            neg_mean, rstd = stats[(1, i)]
            flat = rows[(1, i)][:].rearrange("q g t p -> q (g t p)")
            nc.gpsimd.tensor_scalar(
                out=flat, in0=flat, scalar1=neg_mean[:, 0:1], scalar2=rstd[:, 0:1],
                op0=ALU.add, op1=ALU.mult,
            )

        gate_tiles = [(0, 1), (2, 3), (4, 5), (6,), (7,)]
        gate1 = {}
        h_tiles = {}

        def tokens_of(u):
            return slice(gate_tiles[u][0] * P, (gate_tiles[u][-1] + 1) * P)

        def turn1(u, g):
            tiles = gate_tiles[u]
            columns = PACK // len(tiles)
            for b in range(len(tiles)):
                turned = tp.tile([P, columns, len(tiles) * P], F32, name="turned1", tag="tp")
                for s in range(columns):
                    for j, i in enumerate(tiles):
                        nc.tensor.transpose(
                            turned[:, s, j * P : (j + 1) * P], rows[(1, i)][:, g, columns * b + s, :], ident_f32[:]
                        )
                turned_banks[(1, u, g, b)] = turned

        def gain1(u, g):
            tiles = gate_tiles[u]
            columns = PACK // len(tiles)
            gate1[(u, g)] = stage.tile([P, PACK, len(tiles) * P], F32, name="gate1")
            for t in range(PACK):
                column = g * PACK + t
                nc.scalar.activation(
                    out=gate1[(u, g)][:, t, :], in_=turned_banks[(1, u, g, t // columns)][:, t % columns, :],
                    func=ACT.Identity, scale=affine[:, LN1_G, column : column + 1],
                    bias=affine[:, LN1_B, column : column + 1],
                )

        def multiply(u, g):
            h_tiles[(u, g)] = stage.tile([P, len(gate_tiles[u]) * P, PACK], BF16, align_bytes=64, name="h_grouped")
            nc.vector.tensor_tensor(
                out=h_tiles[(u, g)][:].rearrange("p (c i) t -> p c t i", i=4),
                in0=gate1[(u, g)][:].rearrange("p t (c i) -> p c t i", i=4),
                in1=gate3[:, g * PACK : (g + 1) * PACK, tokens_of(u)].rearrange("p t (c i) -> p c t i", i=4),
                op=ALU.mult,
            )

        def quantise_h(u, g):
            nc.vector.quantize_mx(
                out=h_codes[:, g, tokens_of(u)].bitcast(FP8X4),
                scales=h_scales[:, g, tokens_of(u)],
                in_=h_tiles[(u, g)][:].rearrange("p w t -> p (w t)"),
            )

        def project(i):
            tokens = slice(i * P, (i + 1) * P)
            products[(2, i)] = mx_product(h_codes[:, :, tokens], h_scales[:, :, tokens], c_words, c_planes, "y2")

        def store(i):
            banks = products[(2, i)]
            result = stage.tile([P, BANKS, BANK], F32, name="result", bufs=4)
            for n in range(BANKS):
                nc.vector.tensor_tensor(
                    out=result[:, n, :], in0=banks[n][:],
                    in1=c_b[:, n].rearrange("q t p -> q (t p)"), op=ALU.add,
                )
                if i == TOKEN_TILES - 1:
                    nc.sync.dma_start(
                        out=out_rows[:, i, n * BANK : (n + 1) * BANK], in_=result[:, n, :]
                    )
            if i < TOKEN_TILES - 1:
                nc.sync.dma_start(
                    out=out_rows[:, i, :], in_=result[:].rearrange("q n c -> q (n c)")
                )


        plan = []

        def put(position, stage_function, *which):
            plan.append((position, len(plan), stage_function, which))

        put(-216, turn_z2)
        put(-154, turn_vectors)
        put(-8, turn_u3)
        put(-10, gains_and_shifts)
        put(-150, bias_sums3)
        put(-167, gram3)
        put(-25, gram_bias3)
        for q in range(3):
            put(-8 + 2 * q, forms3, FORM_TILES * q)
        put(2, finish3)
        for half in range(2):
            put(19 + 4 * half, spread_rstd3, half)
        put(-5, spread_row, U1_B, u1_b, "q (p t) -> q t p", ("vector", "scalar"))
        put(-139, spread_row, C_B, c_b, "q (t p) -> q t p", ("scalar", "scalar"))
        for i in range(TOKEN_TILES):
            for lag, stage_function in ((-9, turn_x), (-9, group_x), (-1, quantise_x)):
                put(lag + 3 * i, stage_function, i)
            for lag, stage_function in (
                (9, product1), (11, add_bias1), (14, mean1),
                (14, deviation1), (27, normalise1),
            ):
                put(lag + 4 * i, stage_function, i)
            if i % 4 == 0:
                half = i // 4
                for c in range(PASSES * PACK):
                    for lag, stage_function in ((22, product3), (24, normalise3), (25, gain3)):
                        put(lag + 14 * half + 1.5 * c, stage_function, c, half)
            for u, tiles in enumerate(gate_tiles):
                if tiles[-1] == i:
                    for g in range(PASSES):
                        for lag, stage_function in (
                            (27, turn1), (28, gain1), (32, multiply), (36, quantise_h)
                        ):
                            put(lag + 4 * i + 2 * len(tiles) * g, stage_function, u, g)
                    for j in tiles:
                        put(44 + 4 * j, project, j)
                        put(47 + 4 * j, store, j)
        for position, order, stage_function, which in sorted(plan):
            stage_function(*which)
